import numpy as np
import ml_dtypes


def mxq(x, axis, fmt="e4m3"):
    dtype, down = {"e4m3": (ml_dtypes.float8_e4m3fn, 7), "e5m2": (ml_dtypes.float8_e5m2, 14)}[fmt]
    v = np.moveaxis(np.asarray(x, np.float32).astype(ml_dtypes.bfloat16).astype(np.float64), axis, -1)
    blocks = v.reshape(v.shape[:-1] + (-1, 32))
    amax = np.abs(blocks).max(-1, keepdims=True)
    byte = np.maximum(np.where(amax > 0, np.frexp(amax)[1] - 1 + 127, 0) - down, 1)
    scale = np.exp2(byte - 127.0)
    codes = (blocks / scale).astype(np.float32).astype(dtype).astype(np.float64)
    return np.moveaxis((codes * scale).reshape(v.shape), -1, axis)


WIDE = False


def mx_kscale(k):
    if not WIDE:
        return np.ones(k)
    levels = np.array([18, -18])
    if k % 512:
        return np.exp2(np.random.permutation(np.resize(levels, k // 32))).repeat(32)
    a = np.empty((k // 512, 16))
    for p in range(k // 512):
        a[p, :8] = np.random.permutation(np.resize(levels, 8))
        for g in range(8):
            far = levels[np.abs(levels - a[p, g]) >= 10]
            a[p, g + 8] = far[np.random.randint(len(far))]
    return np.exp2(a.ravel()).repeat(32)


BF16 = ml_dtypes.bfloat16


def bf(x):
    return np.asarray(x, np.float32).astype(BF16)


def f64(x):
    return np.asarray(x).astype(np.float64)


B, C, H, W, ATT_DEPTH, PATCH = 1, 8, 512, 512, 2, 8
DS = 2 ** ATT_DEPTH
HS, WS = H // (PATCH * DS), W // (PATCH * DS)
HT, WT = H // PATCH, W // PATCH
LP, L, N = HS * WS, HT * WT, C * PATCH * PATCH


def setup_inputs():
    s = mx_kscale(L)
    v = mx_kscale(N)
    x0 = bf(np.random.standard_normal((B, C, H, W)) * 2.0 * DS)
    keep = 0.25 + 0.75 * np.random.random((B, 1, L, 1))
    a = (0.1 + 0.9 * np.random.random((B, 1, L, LP))) * (np.random.random((B, 1, L, LP)) < keep)
    a0 = bf(a * 0.3 * np.sqrt(LP))
    nz = np.where(f64(a0) != 0.0, 1.0, 0.0).sum(axis=-1, keepdims=True) + 1e-05
    g = np.random.standard_normal((B, C, HT, PATCH, WT, PATCH)) * 32.0
    g = g * np.exp2(np.random.randint(-6, 1, (B, 1, HT, 1, WT, 1)))
    g = g / s.reshape(1, 1, HT, 1, WT, 1) * v.reshape(1, C, 1, PATCH, 1, PATCH)
    x = f64(x0).reshape(B, C, HS, PATCH, DS, WS, PATCH, DS) / v.reshape(1, C, 1, PATCH, 1, 1, PATCH, 1)
    return {"x": bf(x.reshape(B, C, H, W)), "attentions": bf(f64(a0) * s[:, None]),
            "nz": np.asarray(nz, np.float32), "grad_out": bf(g.reshape(B, C, H, W))}


def reference(x, attentions, nz, grad_out):
    att = f64(attentions).reshape(L, LP)
    pooled = f64(x).reshape(C, H // DS, DS, W // DS, DS).mean(axis=(2, 4))
    u = pooled.reshape(C, HS, PATCH, WS, PATCH).transpose(1, 3, 0, 2, 4).reshape(LP, N)
    go = f64(grad_out).reshape(C, HT, PATCH, WT, PATCH).transpose(1, 3, 0, 2, 4).reshape(L, N)
    dz = go / f64(nz).reshape(L, 1)
    du = mxq(att, 0, "e4m3").T @ mxq(dz, 0, "e5m2")
    da = mxq(dz, 1, "e5m2") @ mxq(u, 1, "e4m3").T
    dp = du.reshape(HS, WS, C, PATCH, PATCH).transpose(2, 0, 3, 1, 4).reshape(C, H // DS, W // DS)
    dx = np.repeat(np.repeat(dp, DS, axis=1), DS, axis=2) / (DS * DS)
    return dx.reshape(B, C, H, W), da.reshape(B, 1, L, LP)

@@ -1,0 +1,412 @@
+from contextlib import ExitStack
+
+import concourse.mybir as mybir
+from concourse.masks import make_identity
+
+F32 = mybir.dt.float32
+BF16 = mybir.dt.bfloat16
+I32 = mybir.dt.int32
+U32 = mybir.dt.uint32
+U8 = mybir.dt.uint8
+E4M3X4 = mybir.dt.float8_e4m3fn_x4
+E5M2X4 = mybir.dt.float8_e5m2_x4
+ALU = mybir.AluOpType
+ACT = mybir.ActivationFunctionType
+
+FLOPS = 2 * 2 * 4096 * 256 * 512
+
+P = 128
+SLOTS = 4
+
+
+def tile_decode_atten_v_kernel(tc, x, attentions, nz, grad_out, out_0, out_1):
+    nc = tc.nc
+
+    grad_rows = grad_out.rearrange("o c (a s m h k) w -> s h k (o c a) m w", a=4, s=2, m=8, h=2, k=4)
+    att_rows = attentions.rearrange("o e (a s p t) j -> s p (o e a) (t j)", a=4, s=2, p=P, t=4)
+    nz_rows = nz.rearrange("o e (g p t) i -> p (o e g) (t i)", g=8, p=P, t=4)
+    x_rows = x.rearrange("o c (q r) w -> (o c) r q w", q=4, r=P)
+    out_0_rows = out_0.rearrange("o c (jh kh a) w -> kh (o c jh) a w", jh=16, kh=8, a=4)
+    out_1_rows = out_1.rearrange("o e (g p t) j -> (o e g) p (t j)", g=8, p=P, t=4)
+
+    with ExitStack() as ctx:
+        keep = ctx.enter_context(tc.tile_pool(name="keep", bufs=1))
+        work = ctx.enter_context(tc.tile_pool(name="work", bufs=1))
+        psum = ctx.enter_context(tc.psum_pool(name="psum", bufs=1))
+        ctx.enter_context(tc.manual_schedule())
+
+        def bank(i):
+            return psum.tile([P, 512], F32, name="bank%d" % i, tag="bank%d" % i)
+
+        def copy(engine, out, in_):
+            if engine == "scalar":
+                nc.scalar.copy(out=out, in_=in_)
+            else:
+                nc.vector.tensor_copy(out=out, in_=in_)
+
+        def times(engine, out, in_, factor):
+            if engine == "scalar":
+                nc.scalar.activation(out=out, in_=in_, func=ACT.Copy, scale=factor)
+            else:
+                nc.vector.tensor_scalar(out=out, in0=in_, scalar1=factor, scalar2=None, op0=ALU.mult)
+
+        nz_sb = keep.tile([P, 8, 4], F32, name="nz_sb")
+        nc.scalar.dma_start(out=nz_sb[:], in_=nz_rows)
+        grad_sb, att_sb, x_sb = {}, {}, {}
+
+        def load_grad(h, s):
+            grad_sb[h, s] = keep.tile([P, 8, 512], BF16, name="grad_sb%d%d" % (h, s))
+            for k in range(4):
+                nc.sync.dma_start(out=grad_sb[h, s][k:P:4, :, :], in_=grad_rows[s, h, k])
+
+        def load_att(s, n):
+            att_sb[s, n] = keep.tile([P, 2, 1024], BF16, name="att_sb%d%d" % (s, n))
+            nc.sync.dma_start(out=att_sb[s, n][:], in_=att_rows[s][:, 2 * n:2 * n + 2, :])
+
+        channels = (0, 2, 4, 6, 1, 3, 5, 7)
+
+        def load_x(i):
+            c = channels[i]
+            x_sb[c] = work.tile([P, 4, 512], BF16, name="x_sb", tag="x_then_da", bufs=8)
+            nc.sync.dma_start(out=x_sb[c][:], in_=x_rows[c])
+
+        load_grad(0, 0)
+        load_att(0, 0)
+        load_grad(0, 1)
+        load_att(0, 1)
+        load_x(0)
+        load_x(1)
+        load_att(1, 0)
+        load_att(1, 1)
+        load_x(2)
+        load_x(3)
+        load_grad(1, 0)
+        load_x(4)
+        load_x(5)
+        load_x(6)
+        load_grad(1, 1)
+        load_x(7)
+
+        ident = keep.tile([P, P], F32, name="ident")
+        make_identity(nc, ident[:])
+        dz_l_codes = keep.tile([P, (2 * SLOTS + 1) * 256], U32, name="dz_l_codes", align_bytes=64)
+        dz_l_scales = keep.tile([P, (2 * SLOTS + 1) * 256], U8, name="dz_l_scales", align_bytes=64)
+        u_codes = keep.tile([P, 768], U32, name="u_codes", align_bytes=64)
+        u_scales = keep.tile([P, 768], U8, name="u_scales", align_bytes=64)
+        for codes, scales in ((dz_l_codes, dz_l_scales), (u_codes, u_scales)):
+            nc.vector.memset(codes[:].rearrange("p (n w) -> p n w", w=256)[:, 0::2, :], 0)
+            nc.vector.memset(scales[:].bitcast(U32).rearrange("p (n w) -> p n w", w=64)[:, 0::2, :], 0)
+        sum4 = keep.tile([P, 32], F32, name="sum4")
+        nc.vector.tensor_reduce(out=sum4[:], in_=ident[:].rearrange("p (r a) -> p r a", a=4),
+                                axis=mybir.AxisListType.X, op=ALU.add)
+        perm_grad = keep.tile([P, P], F32, name="perm_grad")
+        nc.vector.tensor_copy(out=perm_grad[:].rearrange("p (c0 c21 k a) -> p c0 c21 k a", c0=2, c21=4, k=4),
+                              in_=ident[:].rearrange("p (c21 c0 a k) -> p c0 c21 k a", c21=4, c0=2, a=4))
+        perm_du = keep.tile([P, P], F32, name="perm_du")
+        nc.vector.tensor_copy(out=perm_du[:].rearrange("p (jw jh) -> p jw jh", jw=16),
+                              in_=ident[:].rearrange("p (jh jw) -> p jw jh", jw=16))
+        perm_u = keep.tile([P, P], F32, name="perm_u")
+        nc.vector.tensor_copy(out=perm_u[:].rearrange("p (q r v b) -> p q r v b", q=4, r=4, v=2),
+                              in_=ident[:].rearrange("p (b q v r) -> p q r v b", b=4, q=4, v=2))
+        pool_rows = keep.tile([P, 32], BF16, name="pool_rows")
+        times("scalar", pool_rows[:].rearrange("p (kh r) -> p kh r", r=4),
+              sum4[:].rearrange("p (r kh) -> p kh r", r=4), 0.0625)
+        inv_nz = keep.tile([P, 32], F32, name="inv_nz")
+        nc.vector.reciprocal(out=inv_nz[:], in_=nz_sb[:].rearrange("p g t -> p (g t)"))
+
+        dz = [keep.tile([P, 4, 2, 2, 128], BF16, name="dz%d" % g) for g in range(8)]
+        att_codes = [keep.tile([P, 1024], U32, name="att_codes%d" % s, align_bytes=64) for s in range(2)]
+        att_scales = [keep.tile([P, 1024], U8, name="att_scales%d" % s, align_bytes=64) for s in range(2)]
+        live = {}
+
+        def sort_grad(h, s, t):
+            sorted_words = work.tile([P, 4, P], F32, name="sorted_words", bufs=6)
+            words = grad_sb[h, s][:].rearrange("p m w -> p (m w)").bitcast(F32)
+            nc.scalar.copy(out=sorted_words[:].rearrange("p w (mh ml) -> p mh w ml", ml=4),
+                           in_=words.rearrange("p (mh ml t w) -> p t mh w ml", ml=4, t=4, w=4)[:, t])
+            live["sorted", h, s, t] = sorted_words
+
+        def flip_grad(h, s, t, b):
+            flipped = bank(b)
+            for w1 in range(2):
+                for w0 in range(2):
+                    at = (2 * w0 + w1) * P
+                    nc.tensor.transpose(flipped[:, at:at + P], live["sorted", h, s, t][:, 2 * w1 + w0, :], perm_grad[:])
+            live["flipped", h, s, t] = flipped
+
+        def divide(h, s, t, engine):
+            values = live["flipped", h, s, t][:].bitcast(BF16).rearrange(
+                "p (w0 w1 ck a e) -> p a w1 ck w0 e", w0=2, w1=2, ck=32, a=4)
+            for a in range(4):
+                g = 2 * a + s
+                times(engine, dz[g][:, t, :, h, :].rearrange("p w1 (ck w0 e) -> p w1 ck w0 e", w0=2, e=2),
+                      values[:, a], inv_nz[:, 4 * g + t:4 * g + t + 1])
+
+        def weave_dz(h, s, a, engine):
+            woven = work.tile([P, 1024], BF16, name="woven_dz", bufs=4, align_bytes=64)
+            copy(engine, woven[:].rearrange("p (w1 n i t) -> p w1 n t i", w1=2, i=4, t=4),
+                 dz[2 * a + s][:, :, :, h, :].rearrange("p t w1 (n i) -> p w1 n t i", i=4))
+            live["woven_dz", h, s, a] = woven
+
+        def quantize_dz_l(h, s, a):
+            at = (2 * a + 1) * 256
+            nc.vector.quantize_mx(out=dz_l_codes[:, at:at + 256].bitcast(E5M2X4), scales=dz_l_scales[:, at:at + 256],
+                                  in_=live["woven_dz", h, s, a][:])
+
+        def weave_att(s, a):
+            woven = work.tile([P, 1024], BF16, name="woven_att", bufs=4, align_bytes=64)
+            nc.scalar.copy(out=woven[:].rearrange("p (j i t) -> p j t i", i=4, t=4),
+                           in_=att_sb[s, a // 2][:, a % 2, :].rearrange("p (t j i) -> p j t i", t=4, i=4))
+            live["woven_att", s, a] = woven
+
+        def quantize_att(s, a):
+            nc.vector.quantize_mx(out=att_codes[s][:, a * 256:(a + 1) * 256].bitcast(E4M3X4),
+                                  scales=att_scales[s][:, a * 256:(a + 1) * 256], in_=live["woven_att", s, a][:])
+
+        def multiply_l(h, s, a):
+            if s == 0 and a == 0:
+                live["du", h] = bank(h)
+            for half in range(2):
+                js = slice(a * 256 + half * P, a * 256 + (half + 1) * P)
+                at = (2 * a + 1 - half) * 256
+                nc.tensor.matmul_mx(out=live["du", h][:], lhsT=att_codes[s][:, js].bitcast(E4M3X4),
+                                    lhsT_scale=att_scales[s][:, js],
+                                    rhs=dz_l_codes[:, at:at + 512].bitcast(E5M2X4), rhs_scale=dz_l_scales[:, at:at + 512],
+                                    start=(s == 0 and a == 0 and half == 0), stop=(s == 1 and a == 3 and half == 1))
+
+        def copy_du(h):
+            du_sb = work.tile([P, 2, 256], F32, name="du_sb", bufs=1)
+            for half in range(2):
+                nc.scalar.copy(out=du_sb[:, half, :].rearrange("p (c0 ck w1 e) -> p c0 ck w1 e", c0=2, ck=16, w1=2),
+                               in_=live["du", h][:, half * 256:(half + 1) * 256].rearrange(
+                                   "p (w1 c0 ck e) -> p c0 ck w1 e", w1=2, c0=2, ck=16))
+            live["du_sb", h] = du_sb
+
+        def flip_du(h, b):
+            flipped = bank(b)
+            for half in range(2):
+                for c0 in range(2):
+                    nc.tensor.transpose(
+                        flipped[:].rearrange("p (jw c0 half jh) -> p c0 half jw jh", jw=16, c0=2, half=2)[:, c0, half],
+                        live["du_sb", h][:, half, c0 * P:(c0 + 1) * P], perm_du[:])
+            live["du_flipped", h] = flipped
+
+        def swap_du(h):
+            du_rows = work.tile([P, 512], F32, name="du_rows", bufs=2, align_bytes=64)
+            nc.vector.transpose(out=du_rows[:], in_=live["du_flipped", h][:])
+            live["du_rows", h] = du_rows
+
+        def spread_du(h, k, engine):
+            spread = work.tile([P, 512], F32, name="spread", bufs=8)
+            values = live["du_rows", h][:].rearrange("p (jw k kw) -> p k jw kw", jw=16, k=4)[:, k]
+            times(engine, spread[:].rearrange("p (jw kw b) -> p jw kw b", jw=16, kw=8),
+                  values.unsqueeze(3).to_broadcast([P, 16, 8, 4]), 0.0625)
+            nc.sync.dma_start(out=out_0_rows[4 * h + k], in_=spread[:].unsqueeze(1).to_broadcast([P, 4, 512]))
+
+        def pool_x(i):
+            c = channels[i]
+            if i % 2 == 0:
+                live["pooled", i // 2] = bank(4 + i // 2)
+            sums = live["pooled", i // 2][:].rearrange("p (c kh q v r) -> p c q v kh r", c=2, kh=8, q=4, v=2)
+            for q in range(4):
+                for v in range(2):
+                    for b0 in range(2):
+                        nc.tensor.matmul(sums[:, i % 2, q, v], lhsT=x_sb[c][:, q, v * 256 + b0:(v + 1) * 256:2],
+                                         rhs=pool_rows[:].rearrange("p (kh r) -> p kh r", r=4),
+                                         start=(b0 == 0), stop=(b0 == 1))
+
+        pair_sums = keep.tile([P, 2048], F32, name="pair_sums", align_bytes=64)
+        u_bf = keep.tile([P, 1024], BF16, name="u_bf")
+
+        def swap_pooled(n):
+            nc.vector.transpose(out=pair_sums[:, n * 512:(n + 1) * 512], in_=live["pooled", n][:])
+
+        def add_pooled():
+            pairs = pair_sums[:].rearrange("p (c h k v e b) -> p v h b c k e", c=8, h=2, k=4, v=4, e=4)
+            result = u_bf[:].rearrange("p (v h c k e) -> p v h c k e", v=4, h=2, c=8, k=4)
+            for v in range(4):
+                for h in range(2):
+                    nc.vector.tensor_tensor(out=result[:, v, h], in0=pairs[:, v, h, 0], in1=pairs[:, v, h, 1], op=ALU.add)
+
+        def flip_u(b):
+            flipped = bank(b)
+            for v in range(4):
+                nc.tensor.transpose(flipped[:, v * P:(v + 1) * P], u_bf[:].bitcast(F32)[:, v * P:(v + 1) * P], perm_u[:])
+            woven = keep.tile([P, 1024], BF16, name="woven_u", align_bytes=64)
+            nc.scalar.copy(out=woven[:].bitcast(F32).rearrange("p (j v) -> p j v", v=4),
+                           in_=flipped[:].rearrange("p (v j) -> p j v", v=4))
+            live["woven_u"] = woven
+
+        def quantize_u():
+            nc.vector.quantize_mx(out=u_codes[:, 256:512].bitcast(E4M3X4), scales=u_scales[:, 256:512],
+                                  in_=live["woven_u"][:])
+
+        def flip_dz(g, pair, b):
+            flipped = bank(b)
+            words = dz[g][:].rearrange("p t w1 h n -> p (t w1 h n)").bitcast(F32)
+            for n in range(4):
+                at = (4 * pair + n) * P
+                nc.tensor.transpose(flipped[:, n * P:(n + 1) * P], words[:, at:at + P], ident[:])
+            live["dz_flipped", g, pair] = flipped
+
+        def weave_dz_n(g, pair, engine):
+            if pair == 0:
+                live["woven_n", g] = work.tile([P, 2048], BF16, name="woven_n", bufs=4, align_bytes=64)
+            words = live["woven_n", g][:].bitcast(F32)[:, pair * 512:(pair + 1) * 512]
+            copy(engine, words.rearrange("p (t l w1) -> p t l w1", t=2, w1=2),
+                 live["dz_flipped", g, pair][:].rearrange("p (t w1 l) -> p t l w1", t=2, w1=2))
+
+        def quantize_dz_n(g):
+            codes = work.tile([P, 512], U32, name="dz_n_codes", bufs=5, align_bytes=64)
+            scales = work.tile([P, 512], U8, name="dz_n_scales", bufs=5, align_bytes=64)
+            nc.vector.quantize_mx(out=codes[:].bitcast(E5M2X4), scales=scales[:], in_=live["woven_n", g][:])
+            live["dz_n", g] = (codes, scales)
+
+        def multiply_n(g, pair, b):
+            codes, scales = live["dz_n", g]
+            sums = bank(b)
+            for half in range(2):
+                ls = slice((2 * pair + half) * P, (2 * pair + half + 1) * P)
+                at = (1 - half) * 256
+                nc.tensor.matmul_mx(out=sums[:], lhsT=codes[:, ls].bitcast(E5M2X4), lhsT_scale=scales[:, ls],
+                                    rhs=u_codes[:, at:at + 512].bitcast(E4M3X4), rhs_scale=u_scales[:, at:at + 512],
+                                    start=(half == 0), stop=(half == 1))
+            live["da", g, pair] = sums
+
+        def copy_da(g, pair, engine):
+            if pair == 0:
+                live["da_sb", g] = work.tile([P, 1024], F32, name="da_sb", tag="x_then_da", bufs=8)
+            copy(engine, live["da_sb", g][:, pair * 512:(pair + 1) * 512], live["da", g, pair][:])
+            if pair == 1:
+                nc.sync.dma_start(out=out_1_rows[g], in_=live["da_sb", g][:])
+
+        for t in range(4):
+            sort_grad(0, 0, t)
+            flip_grad(0, 0, t, 4 + t)
+            divide(0, 0, t, "vector")
+        weave_att(0, 0)
+        weave_dz(0, 0, 0, "vector")
+        for i in range(4):
+            sort_grad(0, 1, i)
+            if i < 3:
+                weave_att(0, i + 1)
+            flip_grad(0, 1, i, 1 + i % 3)
+            if i > 0:
+                multiply_l(0, 0, i - 1)
+                pool_x(i - 1)
+            if i < 3:
+                weave_dz(0, 0, i + 1, "vector")
+            quantize_dz_l(0, 0, i)
+            quantize_att(0, i)
+            divide(0, 1, i, "vector")
+        multiply_l(0, 0, 3)
+        pool_x(3)
+        weave_att(1, 0)
+        weave_dz(0, 1, 0, "vector")
+        for i in range(4):
+            if i == 2:
+                for t in range(2):
+                    sort_grad(1, 0, t)
+                    flip_grad(1, 0, t, 2 + t)
+            if i < 3:
+                weave_att(1, i + 1)
+                weave_dz(0, 1, i + 1, "vector")
+            quantize_dz_l(0, 1, i)
+            quantize_att(1, i)
+            multiply_l(0, 1, i)
+        sort_grad(1, 0, 2)
+        sort_grad(1, 0, 3)
+        flip_grad(1, 0, 2, 1)
+        copy_du(0)
+        divide(1, 0, 0, "vector")
+        flip_du(0, 0)
+        flip_grad(1, 0, 3, 2)
+        divide(1, 0, 1, "vector")
+        divide(1, 0, 2, "vector")
+        swap_du(0)
+        pool_x(4)
+        pool_x(5)
+        spread_du(0, 0, "scalar")
+        sort_grad(1, 1, 0)
+        sort_grad(1, 1, 1)
+        divide(1, 0, 3, "vector")
+        flip_grad(1, 1, 0, 3)
+        flip_grad(1, 1, 1, 0)
+        sort_grad(1, 1, 2)
+        sort_grad(1, 1, 3)
+        weave_dz(1, 0, 0, "vector")
+        weave_dz(1, 0, 1, "vector")
+        quantize_dz_l(1, 0, 0)
+        flip_grad(1, 1, 2, 2)
+        spread_du(0, 1, "scalar")
+        divide(1, 1, 0, "scalar")
+        weave_dz(1, 0, 2, "vector")
+        quantize_dz_l(1, 0, 1)
+        pool_x(6)
+        multiply_l(1, 0, 0)
+        multiply_l(1, 0, 1)
+        flip_grad(1, 1, 3, 3)
+        pool_x(7)
+        spread_du(0, 2, "scalar")
+        divide(1, 1, 1, "scalar")
+        weave_dz(1, 0, 3, "vector")
+        quantize_dz_l(1, 0, 2)
+        divide(1, 1, 2, "vector")
+        quantize_dz_l(1, 0, 3)
+        divide(1, 1, 3, "vector")
+        spread_du(0, 3, "scalar")
+        multiply_l(1, 0, 2)
+        multiply_l(1, 0, 3)
+        flip_dz(0, 0, 0)
+        weave_dz(1, 1, 0, "vector")
+        weave_dz(1, 1, 3, "scalar")
+        for i in range(4):
+            if i < 2:
+                weave_dz(1, 1, i + 1, "vector")
+            quantize_dz_l(1, 1, i)
+            multiply_l(1, 1, i)
+        weave_dz_n(0, 0, "scalar")
+        flip_dz(0, 1, 2)
+        flip_dz(1, 0, 0)
+        copy_du(1)
+        swap_pooled(0)
+        swap_pooled(1)
+        swap_pooled(2)
+        swap_pooled(3)
+        flip_du(1, 3)
+        weave_dz_n(0, 1, "scalar")
+        flip_dz(1, 1, 2)
+        swap_du(1)
+        weave_dz_n(1, 0, "scalar")
+        spread_du(1, 0, "scalar")
+        add_pooled()
+        quantize_dz_n(0)
+        flip_dz(2, 0, 1)
+        flip_dz(2, 1, 4)
+        flip_dz(3, 0, 5)
+        flip_dz(3, 1, 6)
+        weave_dz_n(1, 1, "scalar")
+        weave_dz_n(2, 0, "scalar")
+        spread_du(1, 1, "scalar")
+        flip_u(7)
+        quantize_dz_n(1)
+        weave_dz_n(2, 1, "vector")
+        quantize_u()
+        quantize_dz_n(2)
+        spread_du(1, 2, "scalar")
+        weave_dz_n(3, 0, "scalar")
+        weave_dz_n(3, 1, "vector")
+        spread_du(1, 3, "scalar")
+        for g in range(8):
+            multiply_n(g, 0, (0, 3)[g % 2])
+            multiply_n(g, 1, (2, 1)[g % 2])
+            if g + 4 < 8:
+                flip_dz(g + 4, 0, 4 + (2 * g) % 4)
+                flip_dz(g + 4, 1, 4 + (2 * g + 1) % 4)
+            if g + 3 < 8:
+                quantize_dz_n(g + 3)
+            copy_da(g, 0, "scalar")
+            copy_da(g, 1, "vector")
+            if g + 4 < 8:
+                weave_dz_n(g + 4, 0, "scalar")
+                weave_dz_n(g + 4, 1, "vector" if g % 2 else "scalar")

@@ -22,7 +22,7 @@ SLOTS = 4
 def tile_decode_atten_v_kernel(tc, x, attentions, nz, grad_out, out_0, out_1):
     nc = tc.nc
 
-    grad_rows = grad_out.rearrange("o c (a s m h k) w -> s h k (o c a) m w", a=4, s=2, m=8, h=2, k=4)
+    grad_rows = grad_out.rearrange("o c (a s m h k) w -> s h m (o c a) k w", a=4, s=2, m=8, h=2, k=4)
     att_rows = attentions.rearrange("o e (a s p t) j -> s p (o e a) (t j)", a=4, s=2, p=P, t=4)
     nz_rows = nz.rearrange("o e (g p t) i -> p (o e g) (t i)", g=8, p=P, t=4)
     x_rows = x.rearrange("o c (q r) w -> (o c) r q w", q=4, r=P)
@@ -51,13 +51,13 @@ def tile_decode_atten_v_kernel(tc, x, attentions, nz, grad_out, out_0, out_1):
                 nc.vector.tensor_scalar(out=out, in0=in_, scalar1=factor, scalar2=None, op0=ALU.mult)
 
         nz_sb = keep.tile([P, 8, 4], F32, name="nz_sb")
-        nc.scalar.dma_start(out=nz_sb[:], in_=nz_rows)
         grad_sb, att_sb, x_sb = {}, {}, {}
 
-        def load_grad(h, s):
-            grad_sb[h, s] = keep.tile([P, 8, 512], BF16, name="grad_sb%d%d" % (h, s))
-            for k in range(4):
-                nc.sync.dma_start(out=grad_sb[h, s][k:P:4, :, :], in_=grad_rows[s, h, k])
+        def load_grad(h, s, first, last):
+            if first == 0:
+                grad_sb[h, s] = keep.tile([P, 8, 512], BF16, name="grad_sb%d%d" % (h, s))
+            for m in range(first, last):
+                nc.sync.dma_start(out=grad_sb[h, s][:, m, :], in_=grad_rows[s, h, m])
 
         def load_att(s, n):
             att_sb[s, n] = keep.tile([P, 2, 1024], BF16, name="att_sb%d%d" % (s, n))
@@ -70,21 +70,25 @@ def tile_decode_atten_v_kernel(tc, x, attentions, nz, grad_out, out_0, out_1):
             x_sb[c] = work.tile([P, 4, 512], BF16, name="x_sb", tag="x_then_da", bufs=8)
             nc.sync.dma_start(out=x_sb[c][:], in_=x_rows[c])
 
-        load_grad(0, 0)
+        load_grad(0, 0, 0, 8)
+        nc.sync.dma_start(out=nz_sb[:], in_=nz_rows)
         load_att(0, 0)
-        load_grad(0, 1)
+        load_grad(0, 1, 0, 8)
         load_att(0, 1)
         load_x(0)
-        load_x(1)
         load_att(1, 0)
+        load_x(1)
         load_att(1, 1)
+        load_grad(1, 0, 0, 3)
         load_x(2)
+        load_grad(1, 0, 3, 6)
         load_x(3)
-        load_grad(1, 0)
+        load_grad(1, 0, 6, 8)
+        load_grad(1, 1, 0, 3)
         load_x(4)
+        load_grad(1, 1, 3, 8)
         load_x(5)
         load_x(6)
-        load_grad(1, 1)
         load_x(7)
 
         ident = keep.tile([P, P], F32, name="ident")
@@ -318,46 +322,45 @@ def tile_decode_atten_v_kernel(tc, x, attentions, nz, grad_out, out_0, out_1):
         sort_grad(1, 0, 3)
         flip_grad(1, 0, 2, 1)
         copy_du(0)
+        sort_grad(1, 1, 0)
+        sort_grad(1, 1, 1)
         divide(1, 0, 0, "vector")
         flip_du(0, 0)
         flip_grad(1, 0, 3, 2)
         divide(1, 0, 1, "vector")
         divide(1, 0, 2, "vector")
         swap_du(0)
-        pool_x(4)
-        pool_x(5)
-        spread_du(0, 0, "scalar")
-        sort_grad(1, 1, 0)
-        sort_grad(1, 1, 1)
-        divide(1, 0, 3, "vector")
         flip_grad(1, 1, 0, 3)
-        flip_grad(1, 1, 1, 0)
+        pool_x(4)
+        spread_du(0, 0, "scalar")
         sort_grad(1, 1, 2)
         sort_grad(1, 1, 3)
+        divide(1, 0, 3, "vector")
+        flip_grad(1, 1, 1, 0)
+        pool_x(5)
+        divide(1, 1, 0, "scalar")
         weave_dz(1, 0, 0, "vector")
         weave_dz(1, 0, 1, "vector")
         quantize_dz_l(1, 0, 0)
         flip_grad(1, 1, 2, 2)
+        flip_grad(1, 1, 3, 3)
         spread_du(0, 1, "scalar")
-        divide(1, 1, 0, "scalar")
+        divide(1, 1, 1, "scalar")
         weave_dz(1, 0, 2, "vector")
         quantize_dz_l(1, 0, 1)
-        pool_x(6)
         multiply_l(1, 0, 0)
         multiply_l(1, 0, 1)
-        flip_grad(1, 1, 3, 3)
-        pool_x(7)
+        pool_x(6)
         spread_du(0, 2, "scalar")
-        divide(1, 1, 1, "scalar")
+        divide(1, 1, 2, "scalar")
         weave_dz(1, 0, 3, "vector")
         quantize_dz_l(1, 0, 2)
-        divide(1, 1, 2, "vector")
-        quantize_dz_l(1, 0, 3)
         divide(1, 1, 3, "vector")
+        quantize_dz_l(1, 0, 3)
         spread_du(0, 3, "scalar")
         multiply_l(1, 0, 2)
         multiply_l(1, 0, 3)
-        flip_dz(0, 0, 0)
+        swap_pooled(0)
         weave_dz(1, 1, 0, "vector")
         weave_dz(1, 1, 3, "scalar")
         for i in range(4):
@@ -365,48 +368,44 @@ def tile_decode_atten_v_kernel(tc, x, attentions, nz, grad_out, out_0, out_1):
                 weave_dz(1, 1, i + 1, "vector")
             quantize_dz_l(1, 1, i)
             multiply_l(1, 1, i)
-        weave_dz_n(0, 0, "scalar")
-        flip_dz(0, 1, 2)
-        flip_dz(1, 0, 0)
         copy_du(1)
-        swap_pooled(0)
+        pool_x(7)
         swap_pooled(1)
         swap_pooled(2)
-        swap_pooled(3)
         flip_du(1, 3)
-        weave_dz_n(0, 1, "scalar")
-        flip_dz(1, 1, 2)
+        flip_dz(0, 0, 0)
+        flip_dz(0, 1, 2)
+        flip_dz(1, 0, 4)
+        flip_dz(1, 1, 5)
         swap_du(1)
-        weave_dz_n(1, 0, "scalar")
+        swap_pooled(3)
+        weave_dz_n(0, 0, "scalar")
         spread_du(1, 0, "scalar")
         add_pooled()
-        quantize_dz_n(0)
+        weave_dz_n(0, 1, "scalar")
         flip_dz(2, 0, 1)
-        flip_dz(2, 1, 4)
-        flip_dz(3, 0, 5)
-        flip_dz(3, 1, 6)
-        weave_dz_n(1, 1, "scalar")
-        weave_dz_n(2, 0, "scalar")
-        spread_du(1, 1, "scalar")
-        flip_u(7)
-        quantize_dz_n(1)
-        weave_dz_n(2, 1, "vector")
+        flip_dz(2, 1, 6)
+        flip_u(0)
+        weave_dz_n(1, 0, "vector")
+        quantize_dz_n(0)
         quantize_u()
-        quantize_dz_n(2)
-        spread_du(1, 2, "scalar")
-        weave_dz_n(3, 0, "scalar")
-        weave_dz_n(3, 1, "vector")
-        spread_du(1, 3, "scalar")
+        spread_du(1, 1, "scalar")
+        weave_dz_n(1, 1, "scalar")
+        weave_dz_n(2, 0, "vector")
+        weave_dz_n(2, 1, "vector")
+        quantize_dz_n(1)
         for g in range(8):
             multiply_n(g, 0, (0, 3)[g % 2])
             multiply_n(g, 1, (2, 1)[g % 2])
-            if g + 4 < 8:
-                flip_dz(g + 4, 0, 4 + (2 * g) % 4)
-                flip_dz(g + 4, 1, 4 + (2 * g + 1) % 4)
             if g + 3 < 8:
-                quantize_dz_n(g + 3)
+                flip_dz(g + 3, 0, 4 + (2 * g + 3) % 4)
+                flip_dz(g + 3, 1, 4 + (2 * g) % 4)
+            if g < 2:
+                spread_du(1, 2 + g, "scalar")
+            if g + 2 < 8:
+                quantize_dz_n(g + 2)
             copy_da(g, 0, "scalar")
             copy_da(g, 1, "vector")
-            if g + 4 < 8:
-                weave_dz_n(g + 4, 0, "scalar")
-                weave_dz_n(g + 4, 1, "vector" if g % 2 else "scalar")
+            if g + 3 < 8:
+                weave_dz_n(g + 3, 0, "scalar")
+                weave_dz_n(g + 3, 1, "vector" if g % 2 == 0 else "scalar")

@@ -63,33 +63,27 @@ def tile_decode_atten_v_kernel(tc, x, attentions, nz, grad_out, out_0, out_1):
             att_sb[s, n] = keep.tile([P, 2, 1024], BF16, name="att_sb%d%d" % (s, n))
             nc.sync.dma_start(out=att_sb[s, n][:], in_=att_rows[s][:, 2 * n:2 * n + 2, :])
 
-        channels = (0, 2, 4, 6, 1, 3, 5, 7)
 
-        def load_x(i):
-            c = channels[i]
+        def load_x(c):
             x_sb[c] = work.tile([P, 4, 512], BF16, name="x_sb", tag="x_then_da", bufs=8)
             nc.sync.dma_start(out=x_sb[c][:], in_=x_rows[c])
 
         load_grad(0, 0, 0, 8)
         nc.sync.dma_start(out=nz_sb[:], in_=nz_rows)
         load_att(0, 0)
+        load_x(0)
         load_grad(0, 1, 0, 8)
         load_att(0, 1)
-        load_x(0)
-        load_att(1, 0)
         load_x(1)
-        load_att(1, 1)
-        load_grad(1, 0, 0, 3)
         load_x(2)
-        load_grad(1, 0, 3, 6)
+        load_att(1, 0)
+        load_grad(1, 0, 0, 8)
         load_x(3)
-        load_grad(1, 0, 6, 8)
-        load_grad(1, 1, 0, 3)
+        load_att(1, 1)
         load_x(4)
-        load_grad(1, 1, 3, 8)
-        load_x(5)
-        load_x(6)
-        load_x(7)
+        load_grad(1, 1, 0, 8)
+        for c in range(5, 8):
+            load_x(c)
 
         ident = keep.tile([P, P], F32, name="ident")
         make_identity(nc, ident[:])
@@ -103,9 +97,6 @@ def tile_decode_atten_v_kernel(tc, x, attentions, nz, grad_out, out_0, out_1):
         sum4 = keep.tile([P, 32], F32, name="sum4")
         nc.vector.tensor_reduce(out=sum4[:], in_=ident[:].rearrange("p (r a) -> p r a", a=4),
                                 axis=mybir.AxisListType.X, op=ALU.add)
-        perm_grad = keep.tile([P, P], F32, name="perm_grad")
-        nc.vector.tensor_copy(out=perm_grad[:].rearrange("p (c0 c21 k a) -> p c0 c21 k a", c0=2, c21=4, k=4),
-                              in_=ident[:].rearrange("p (c21 c0 a k) -> p c0 c21 k a", c21=4, c0=2, a=4))
         perm_du = keep.tile([P, P], F32, name="perm_du")
         nc.vector.tensor_copy(out=perm_du[:].rearrange("p (jw jh) -> p jw jh", jw=16),
                               in_=ident[:].rearrange("p (jh jw) -> p jw jh", jw=16))
@@ -135,21 +126,21 @@ def tile_decode_atten_v_kernel(tc, x, attentions, nz, grad_out, out_0, out_1):
             for w1 in range(2):
                 for w0 in range(2):
                     at = (2 * w0 + w1) * P
-                    nc.tensor.transpose(flipped[:, at:at + P], live["sorted", h, s, t][:, 2 * w1 + w0, :], perm_grad[:])
+                    nc.tensor.transpose(flipped[:, at:at + P], live["sorted", h, s, t][:, 2 * w1 + w0, :], ident[:])
             live["flipped", h, s, t] = flipped
 
         def divide(h, s, t, engine):
             values = live["flipped", h, s, t][:].bitcast(BF16).rearrange(
-                "p (w0 w1 ck a e) -> p a w1 ck w0 e", w0=2, w1=2, ck=32, a=4)
+                "p (w0 w1 c a ke) -> p a w1 c w0 ke", w0=2, w1=2, c=8, a=4)
             for a in range(4):
                 g = 2 * a + s
-                times(engine, dz[g][:, t, :, h, :].rearrange("p w1 (ck w0 e) -> p w1 ck w0 e", w0=2, e=2),
+                times(engine, dz[g][:, t, :, h, :].rearrange("p w1 (c w0 ke) -> p w1 c w0 ke", c=8, w0=2),
                       values[:, a], inv_nz[:, 4 * g + t:4 * g + t + 1])
 
         def weave_dz(h, s, a, engine):
             woven = work.tile([P, 1024], BF16, name="woven_dz", bufs=4, align_bytes=64)
-            copy(engine, woven[:].rearrange("p (w1 n i t) -> p w1 n t i", w1=2, i=4, t=4),
-                 dz[2 * a + s][:, :, :, h, :].rearrange("p t w1 (n i) -> p w1 n t i", i=4))
+            copy(engine, woven[:].rearrange("p (w1 n t) -> p w1 n t", w1=2, t=4),
+                 dz[2 * a + s][:, :, :, h, :].rearrange("p t w1 n -> p w1 n t"))
             live["woven_dz", h, s, a] = woven
 
         def quantize_dz_l(h, s, a):
@@ -159,8 +150,8 @@ def tile_decode_atten_v_kernel(tc, x, attentions, nz, grad_out, out_0, out_1):
 
         def weave_att(s, a):
             woven = work.tile([P, 1024], BF16, name="woven_att", bufs=4, align_bytes=64)
-            nc.scalar.copy(out=woven[:].rearrange("p (j i t) -> p j t i", i=4, t=4),
-                           in_=att_sb[s, a // 2][:, a % 2, :].rearrange("p (t j i) -> p j t i", t=4, i=4))
+            nc.scalar.copy(out=woven[:].rearrange("p (j t) -> p j t", t=4),
+                           in_=att_sb[s, a // 2][:, a % 2, :].rearrange("p (t j) -> p j t", t=4))
             live["woven_att", s, a] = woven
 
         def quantize_att(s, a):
@@ -181,9 +172,9 @@ def tile_decode_atten_v_kernel(tc, x, attentions, nz, grad_out, out_0, out_1):
         def copy_du(h):
             du_sb = work.tile([P, 2, 256], F32, name="du_sb", bufs=1)
             for half in range(2):
-                nc.scalar.copy(out=du_sb[:, half, :].rearrange("p (c0 ck w1 e) -> p c0 ck w1 e", c0=2, ck=16, w1=2),
+                nc.scalar.copy(out=du_sb[:, half, :].rearrange("p (c0 c21 w1 r) -> p c0 c21 w1 r", c0=2, c21=4, w1=2),
                                in_=live["du", h][:, half * 256:(half + 1) * 256].rearrange(
-                                   "p (w1 c0 ck e) -> p c0 ck w1 e", w1=2, c0=2, ck=16))
+                                   "p (w1 c21 c0 r) -> p c0 c21 w1 r", w1=2, c21=4, c0=2))
             live["du_sb", h] = du_sb
 
         def flip_du(h, b):
@@ -202,20 +193,19 @@ def tile_decode_atten_v_kernel(tc, x, attentions, nz, grad_out, out_0, out_1):
 
         def spread_du(h, k, engine):
             spread = work.tile([P, 512], F32, name="spread", bufs=8)
-            values = live["du_rows", h][:].rearrange("p (jw k kw) -> p k jw kw", jw=16, k=4)[:, k]
-            times(engine, spread[:].rearrange("p (jw kw b) -> p jw kw b", jw=16, kw=8),
-                  values.unsqueeze(3).to_broadcast([P, 16, 8, 4]), 0.0625)
+            values = live["du_rows", h][:].rearrange("p (pair k e) -> p k pair e", k=4, e=2)[:, k]
+            times(engine, spread[:].rearrange("p (pair e b) -> p pair e b", e=2, b=4),
+                  values.unsqueeze(3).to_broadcast([P, 64, 2, 4]), 0.0625)
             nc.sync.dma_start(out=out_0_rows[4 * h + k], in_=spread[:].unsqueeze(1).to_broadcast([P, 4, 512]))
 
-        def pool_x(i):
-            c = channels[i]
-            if i % 2 == 0:
-                live["pooled", i // 2] = bank(4 + i // 2)
-            sums = live["pooled", i // 2][:].rearrange("p (c kh q v r) -> p c q v kh r", c=2, kh=8, q=4, v=2)
+        def pool_x(c):
+            if c % 2 == 0:
+                live["pooled", c // 2] = bank(4 + c // 2)
+            sums = live["pooled", c // 2][:].rearrange("p (c kh q v r) -> p c q v kh r", c=2, kh=8, q=4, v=2)
             for q in range(4):
                 for v in range(2):
                     for b0 in range(2):
-                        nc.tensor.matmul(sums[:, i % 2, q, v], lhsT=x_sb[c][:, q, v * 256 + b0:(v + 1) * 256:2],
+                        nc.tensor.matmul(sums[:, c % 2, q, v], lhsT=x_sb[c][:, q, v * 256 + b0:(v + 1) * 256:2],
                                          rhs=pool_rows[:].rearrange("p (kh r) -> p kh r", r=4),
                                          start=(b0 == 0), stop=(b0 == 1))
 
@@ -226,11 +216,12 @@ def tile_decode_atten_v_kernel(tc, x, attentions, nz, grad_out, out_0, out_1):
             nc.vector.transpose(out=pair_sums[:, n * 512:(n + 1) * 512], in_=live["pooled", n][:])
 
         def add_pooled():
-            pairs = pair_sums[:].rearrange("p (c h k v e b) -> p v h b c k e", c=8, h=2, k=4, v=4, e=4)
-            result = u_bf[:].rearrange("p (v h c k e) -> p v h c k e", v=4, h=2, c=8, k=4)
+            pairs = pair_sums[:].rearrange("p (c h k v w0 e b) -> p v w0 b c h k e", c=8, h=2, k=4, v=4, w0=2, e=2)
+            result = u_bf[:].rearrange("p (v h c w0 k e) -> p v w0 c h k e", v=4, h=2, c=8, w0=2, k=4)
             for v in range(4):
-                for h in range(2):
-                    nc.vector.tensor_tensor(out=result[:, v, h], in0=pairs[:, v, h, 0], in1=pairs[:, v, h, 1], op=ALU.add)
+                for w0 in range(2):
+                    nc.vector.tensor_tensor(out=result[:, v, w0], in0=pairs[:, v, w0, 0], in1=pairs[:, v, w0, 1],
+                                            op=ALU.add)
 
         def flip_u(b):
             flipped = bank(b)
@@ -284,83 +275,68 @@ def tile_decode_atten_v_kernel(tc, x, attentions, nz, grad_out, out_0, out_1):
             if pair == 1:
                 nc.sync.dma_start(out=out_1_rows[g], in_=live["da_sb", g][:])
 
+        units = ((0, 0), (0, 1), (1, 0))
+        flip_banks = ((4, 5, 6, 7), (1, 2, 3, 1), (2, 3, 1, 2))
         for t in range(4):
             sort_grad(0, 0, t)
-            flip_grad(0, 0, t, 4 + t)
+            flip_grad(0, 0, t, flip_banks[0][t])
             divide(0, 0, t, "vector")
+        pool_x(0)
         weave_att(0, 0)
         weave_dz(0, 0, 0, "vector")
-        for i in range(4):
-            sort_grad(0, 1, i)
+        for step in range(8):
+            s, i = divmod(step, 4)
+            if step == 0:
+                weave_att(0, 1)
+            sort_grad(*units[s + 1], i)
+            if 0 < step < 7:
+                weave_att(*divmod(step + 1, 4))
+            flip_grad(*units[s + 1], i, flip_banks[s + 1][i])
+            if step > 0:
+                multiply_l(0, *divmod(step - 1, 4))
+            if step in (1, 2, 4, 5):
+                pool_x(1 + (1, 2, 4, 5).index(step))
             if i < 3:
-                weave_att(0, i + 1)
-            flip_grad(0, 1, i, 1 + i % 3)
-            if i > 0:
-                multiply_l(0, 0, i - 1)
-                pool_x(i - 1)
-            if i < 3:
-                weave_dz(0, 0, i + 1, "vector")
-            quantize_dz_l(0, 0, i)
-            quantize_att(0, i)
-            divide(0, 1, i, "vector")
-        multiply_l(0, 0, 3)
-        pool_x(3)
-        weave_att(1, 0)
-        weave_dz(0, 1, 0, "vector")
-        for i in range(4):
-            if i == 2:
-                for t in range(2):
-                    sort_grad(1, 0, t)
-                    flip_grad(1, 0, t, 2 + t)
-            if i < 3:
-                weave_att(1, i + 1)
-                weave_dz(0, 1, i + 1, "vector")
-            quantize_dz_l(0, 1, i)
-            quantize_att(1, i)
-            multiply_l(0, 1, i)
-        sort_grad(1, 0, 2)
-        sort_grad(1, 0, 3)
-        flip_grad(1, 0, 2, 1)
+                weave_dz(0, s, i + 1, "vector")
+            quantize_dz_l(0, s, i)
+            quantize_att(s, i)
+            if step < 6:
+                divide(*units[s + 1], i, "vector")
+            if step == 3:
+                weave_dz(0, 1, 0, "vector")
+        multiply_l(0, 1, 3)
+        for t in range(4):
+            sort_grad(1, 1, t)
         copy_du(0)
-        sort_grad(1, 1, 0)
-        sort_grad(1, 1, 1)
-        divide(1, 0, 0, "vector")
-        flip_du(0, 0)
-        flip_grad(1, 0, 3, 2)
-        divide(1, 0, 1, "vector")
-        divide(1, 0, 2, "vector")
-        swap_du(0)
         flip_grad(1, 1, 0, 3)
-        pool_x(4)
-        spread_du(0, 0, "scalar")
-        sort_grad(1, 1, 2)
-        sort_grad(1, 1, 3)
+        flip_grad(1, 1, 1, 7)
+        flip_du(0, 0)
+        divide(1, 0, 2, "vector")
         divide(1, 0, 3, "vector")
-        flip_grad(1, 1, 1, 0)
         pool_x(5)
         divide(1, 1, 0, "scalar")
-        weave_dz(1, 0, 0, "vector")
-        weave_dz(1, 0, 1, "vector")
-        quantize_dz_l(1, 0, 0)
         flip_grad(1, 1, 2, 2)
         flip_grad(1, 1, 3, 3)
-        spread_du(0, 1, "scalar")
+        weave_dz(1, 0, 0, "vector")
+        swap_du(0)
+        weave_dz(1, 0, 1, "vector")
+        quantize_dz_l(1, 0, 0)
+        spread_du(0, 0, "scalar")
         divide(1, 1, 1, "scalar")
-        weave_dz(1, 0, 2, "vector")
-        quantize_dz_l(1, 0, 1)
-        multiply_l(1, 0, 0)
-        multiply_l(1, 0, 1)
-        pool_x(6)
-        spread_du(0, 2, "scalar")
-        divide(1, 1, 2, "scalar")
-        weave_dz(1, 0, 3, "vector")
-        quantize_dz_l(1, 0, 2)
-        divide(1, 1, 3, "vector")
-        quantize_dz_l(1, 0, 3)
-        spread_du(0, 3, "scalar")
-        multiply_l(1, 0, 2)
+        for i in range(1, 4):
+            multiply_l(1, 0, i - 1)
+            if i == 2:
+                pool_x(6)
+            if i < 3:
+                weave_dz(1, 0, i + 1, "vector")
+            else:
+                divide(1, 1, 3, "vector")
+            quantize_dz_l(1, 0, i)
+            spread_du(0, i, "scalar")
+            if i == 1:
+                divide(1, 1, 2, "scalar")
         multiply_l(1, 0, 3)
-        swap_pooled(0)
+        pool_x(7)
         weave_dz(1, 1, 0, "vector")
         weave_dz(1, 1, 3, "scalar")
         for i in range(4):
@@ -369,27 +345,25 @@ def tile_decode_atten_v_kernel(tc, x, attentions, nz, grad_out, out_0, out_1):
             quantize_dz_l(1, 1, i)
             multiply_l(1, 1, i)
         copy_du(1)
-        pool_x(7)
-        swap_pooled(1)
-        swap_pooled(2)
-        flip_du(1, 3)
+        for n in range(4):
+            swap_pooled(n)
         flip_dz(0, 0, 0)
         flip_dz(0, 1, 2)
+        flip_du(1, 3)
         flip_dz(1, 0, 4)
         flip_dz(1, 1, 5)
-        swap_du(1)
-        swap_pooled(3)
         weave_dz_n(0, 0, "scalar")
-        spread_du(1, 0, "scalar")
+        swap_du(1)
         add_pooled()
+        spread_du(1, 0, "scalar")
         weave_dz_n(0, 1, "scalar")
         flip_dz(2, 0, 1)
         flip_dz(2, 1, 6)
         flip_u(0)
+        spread_du(1, 1, "scalar")
         weave_dz_n(1, 0, "vector")
         quantize_dz_n(0)
         quantize_u()
-        spread_du(1, 1, "scalar")
         weave_dz_n(1, 1, "scalar")
         weave_dz_n(2, 0, "vector")
         weave_dz_n(2, 1, "vector")

@@ -24,9 +24,9 @@ def tile_decode_atten_v_kernel(tc, x, attentions, nz, grad_out, out_0, out_1):
 
     grad_rows = grad_out.rearrange("o c (a s m h k) w -> s h m (o c a) k w", a=4, s=2, m=8, h=2, k=4)
     att_rows = attentions.rearrange("o e (a s p t) j -> s p (o e a) (t j)", a=4, s=2, p=P, t=4)
-    nz_rows = nz.rearrange("o e (g p t) i -> p (o e g) (t i)", g=8, p=P, t=4)
+    nz_rows = nz.rearrange("o e (g l) i -> (o e g) (l i)", g=8)
     x_rows = x.rearrange("o c (q r) w -> (o c) r q w", q=4, r=P)
-    out_0_rows = out_0.rearrange("o c (jh kh a) w -> kh (o c jh) a w", jh=16, kh=8, a=4)
+    out_0_rows = out_0.rearrange("o c (jh kh a r) w -> kh (o c jh) a (r w)", jh=16, kh=8, a=2, r=2)
     out_1_rows = out_1.rearrange("o e (g p t) j -> (o e g) p (t j)", g=8, p=P, t=4)
 
     with ExitStack() as ctx:
@@ -50,7 +50,8 @@ def tile_decode_atten_v_kernel(tc, x, attentions, nz, grad_out, out_0, out_1):
             else:
                 nc.vector.tensor_scalar(out=out, in0=in_, scalar1=factor, scalar2=None, op0=ALU.mult)
 
-        nz_sb = keep.tile([P, 8, 4], F32, name="nz_sb")
+        nz_sb = keep.tile([P, 512], F32, name="nz_sb")
+        nc.vector.memset(nz_sb[:], 0.0)
         grad_sb, att_sb, x_sb = {}, {}, {}
 
         def load_grad(h, s, first, last):
@@ -69,20 +70,18 @@ def tile_decode_atten_v_kernel(tc, x, attentions, nz, grad_out, out_0, out_1):
             nc.sync.dma_start(out=x_sb[c][:], in_=x_rows[c])
 
         load_grad(0, 0, 0, 8)
-        nc.sync.dma_start(out=nz_sb[:], in_=nz_rows)
+        nc.sync.dma_start(out=nz_sb[0:8, :], in_=nz_rows)
         load_att(0, 0)
-        load_x(0)
         load_grad(0, 1, 0, 8)
         load_att(0, 1)
+        load_att(1, 0)
+        load_x(0)
+        load_grad(1, 0, 0, 8)
+        load_att(1, 1)
         load_x(1)
         load_x(2)
-        load_att(1, 0)
-        load_grad(1, 0, 0, 8)
-        load_x(3)
-        load_att(1, 1)
-        load_x(4)
         load_grad(1, 1, 0, 8)
-        for c in range(5, 8):
+        for c in range(3, 8):
             load_x(c)
 
         ident = keep.tile([P, P], F32, name="ident")
@@ -107,7 +106,11 @@ def tile_decode_atten_v_kernel(tc, x, attentions, nz, grad_out, out_0, out_1):
         times("scalar", pool_rows[:].rearrange("p (kh r) -> p kh r", r=4),
               sum4[:].rearrange("p (r kh) -> p kh r", r=4), 0.0625)
         inv_nz = keep.tile([P, 32], F32, name="inv_nz")
-        nc.vector.reciprocal(out=inv_nz[:], in_=nz_sb[:].rearrange("p g t -> p (g t)"))
+        nz_flipped = bank(1)
+        for t in range(4):
+            nc.tensor.transpose(nz_flipped[:, t * P:(t + 1) * P], nz_sb[:, t:512:4], ident[:])
+        nc.vector.reciprocal(out=inv_nz[:].rearrange("p (g t) -> p t g", t=4),
+                             in_=nz_flipped[:].rearrange("p (t g) -> p t g", t=4)[:, :, 0:8])
 
         dz = [keep.tile([P, 4, 2, 2, 128], BF16, name="dz%d" % g) for g in range(8)]
         att_codes = [keep.tile([P, 1024], U32, name="att_codes%d" % s, align_bytes=64) for s in range(2)]
@@ -192,11 +195,13 @@ def tile_decode_atten_v_kernel(tc, x, attentions, nz, grad_out, out_0, out_1):
             live["du_rows", h] = du_rows
 
         def spread_du(h, k, engine):
-            spread = work.tile([P, 512], F32, name="spread", bufs=8)
+            spread = work.tile([P, 2, 512], F32, name="spread", bufs=5)
             values = live["du_rows", h][:].rearrange("p (pair k e) -> p k pair e", k=4, e=2)[:, k]
-            times(engine, spread[:].rearrange("p (pair e b) -> p pair e b", e=2, b=4),
-                  values.unsqueeze(3).to_broadcast([P, 64, 2, 4]), 0.0625)
-            nc.sync.dma_start(out=out_0_rows[4 * h + k], in_=spread[:].unsqueeze(1).to_broadcast([P, 4, 512]))
+            for row in range(2):
+                times(engine[row], spread[:, row, :].rearrange("p (pair e b) -> p pair e b", e=2, b=4),
+                      values.unsqueeze(3).to_broadcast([P, 64, 2, 4]), 0.0625)
+            nc.sync.dma_start(out=out_0_rows[4 * h + k],
+                              in_=spread[:].rearrange("p r w -> p (r w)").unsqueeze(1).to_broadcast([P, 2, 1024]))
 
         def pool_x(c):
             if c % 2 == 0:
@@ -275,98 +280,95 @@ def tile_decode_atten_v_kernel(tc, x, attentions, nz, grad_out, out_0, out_1):
             if pair == 1:
                 nc.sync.dma_start(out=out_1_rows[g], in_=live["da_sb", g][:])
 
+        both = ("scalar", "vector")
         units = ((0, 0), (0, 1), (1, 0))
         flip_banks = ((4, 5, 6, 7), (1, 2, 3, 1), (2, 3, 1, 2))
         for t in range(4):
             sort_grad(0, 0, t)
             flip_grad(0, 0, t, flip_banks[0][t])
             divide(0, 0, t, "vector")
-        pool_x(0)
         weave_att(0, 0)
         weave_dz(0, 0, 0, "vector")
         for step in range(8):
             s, i = divmod(step, 4)
-            if step == 0:
-                weave_att(0, 1)
             sort_grad(*units[s + 1], i)
-            if 0 < step < 7:
+            if step < 7:
                 weave_att(*divmod(step + 1, 4))
             flip_grad(*units[s + 1], i, flip_banks[s + 1][i])
             if step > 0:
                 multiply_l(0, *divmod(step - 1, 4))
-            if step in (1, 2, 4, 5):
-                pool_x(1 + (1, 2, 4, 5).index(step))
+            if step in (2, 5, 6):
+                pool_x((2, 5, 6).index(step))
             if i < 3:
                 weave_dz(0, s, i + 1, "vector")
             quantize_dz_l(0, s, i)
             quantize_att(s, i)
-            if step < 6:
-                divide(*units[s + 1], i, "vector")
-            if step == 3:
-                weave_dz(0, 1, 0, "vector")
+            divide(*units[s + 1], i, "vector")
+            if i == 3:
+                weave_dz(*units[s + 1], 0, "vector")
         multiply_l(0, 1, 3)
-        for t in range(4):
-            sort_grad(1, 1, t)
+        sort_grad(1, 1, 0)
+        sort_grad(1, 1, 1)
         copy_du(0)
+        sort_grad(1, 1, 2)
+        sort_grad(1, 1, 3)
         flip_grad(1, 1, 0, 3)
         flip_grad(1, 1, 1, 7)
         flip_du(0, 0)
-        divide(1, 0, 2, "vector")
-        divide(1, 0, 3, "vector")
-        pool_x(5)
-        divide(1, 1, 0, "scalar")
         flip_grad(1, 1, 2, 2)
-        flip_grad(1, 1, 3, 3)
-        weave_dz(1, 0, 0, "vector")
-        swap_du(0)
+        pool_x(3)
         weave_dz(1, 0, 1, "vector")
         quantize_dz_l(1, 0, 0)
-        spread_du(0, 0, "scalar")
-        divide(1, 1, 1, "scalar")
+        divide(1, 1, 0, "vector")
+        swap_du(0)
+        flip_grad(1, 1, 3, 3)
         for i in range(1, 4):
+            spread_du(0, i - 1, both)
             multiply_l(1, 0, i - 1)
-            if i == 2:
-                pool_x(6)
+            if i > 1:
+                pool_x(2 + i)
             if i < 3:
                 weave_dz(1, 0, i + 1, "vector")
+                divide(1, 1, i, "scalar")
             else:
                 divide(1, 1, 3, "vector")
             quantize_dz_l(1, 0, i)
-            spread_du(0, i, "scalar")
-            if i == 1:
-                divide(1, 1, 2, "scalar")
         multiply_l(1, 0, 3)
-        pool_x(7)
         weave_dz(1, 1, 0, "vector")
         weave_dz(1, 1, 3, "scalar")
+        spread_du(0, 3, ("scalar", "scalar"))
         for i in range(4):
             if i < 2:
                 weave_dz(1, 1, i + 1, "vector")
             quantize_dz_l(1, 1, i)
             multiply_l(1, 1, i)
         copy_du(1)
-        for n in range(4):
-            swap_pooled(n)
+        pool_x(6)
+        swap_pooled(0)
+        swap_pooled(1)
+        swap_pooled(2)
+        flip_du(1, 3)
+        pool_x(7)
         flip_dz(0, 0, 0)
         flip_dz(0, 1, 2)
-        flip_du(1, 3)
         flip_dz(1, 0, 4)
         flip_dz(1, 1, 5)
-        weave_dz_n(0, 0, "scalar")
         swap_du(1)
+        spread_du(1, 0, both)
+        swap_pooled(3)
+        weave_dz_n(0, 0, "scalar")
+        spread_du(1, 1, both)
         add_pooled()
-        spread_du(1, 0, "scalar")
         weave_dz_n(0, 1, "scalar")
         flip_dz(2, 0, 1)
         flip_dz(2, 1, 6)
         flip_u(0)
-        spread_du(1, 1, "scalar")
         weave_dz_n(1, 0, "vector")
         quantize_dz_n(0)
         quantize_u()
         weave_dz_n(1, 1, "scalar")
         weave_dz_n(2, 0, "vector")
-        weave_dz_n(2, 1, "vector")
+        weave_dz_n(2, 1, "scalar")
         quantize_dz_n(1)
         for g in range(8):
             multiply_n(g, 0, (0, 3)[g % 2])
@@ -375,7 +377,7 @@ def tile_decode_atten_v_kernel(tc, x, attentions, nz, grad_out, out_0, out_1):
                 flip_dz(g + 3, 0, 4 + (2 * g + 3) % 4)
                 flip_dz(g + 3, 1, 4 + (2 * g) % 4)
             if g < 2:
-                spread_du(1, 2 + g, "scalar")
+                spread_du(1, 2 + g, both)
             if g + 2 < 8:
                 quantize_dz_n(g + 2)
             copy_da(g, 0, "scalar")

@@ -5,7 +5,6 @@ from concourse.masks import make_identity
 
 F32 = mybir.dt.float32
 BF16 = mybir.dt.bfloat16
-I32 = mybir.dt.int32
 U32 = mybir.dt.uint32
 U8 = mybir.dt.uint8
 E4M3X4 = mybir.dt.float8_e4m3fn_x4
@@ -16,7 +15,12 @@ ACT = mybir.ActivationFunctionType
 FLOPS = 2 * 2 * 4096 * 256 * 512
 
 P = 128
-SLOTS = 4
+CHANNELS = 8
+PASSES = 8
+HALF_BANK = 256
+MEAN_16 = 0.0625
+FIRST_PAIRED = 4
+FIRST_POOL_BANK = 4
 
 
 def tile_decode_atten_v_kernel(tc, x, attentions, nz, grad_out, out_0, out_1):
@@ -24,10 +28,11 @@ def tile_decode_atten_v_kernel(tc, x, attentions, nz, grad_out, out_0, out_1):
 
     grad_rows = grad_out.rearrange("o c (a s m h k) w -> s h m (o c a) k w", a=4, s=2, m=8, h=2, k=4)
     att_rows = attentions.rearrange("o e (a s p t) j -> s p (o e a) (t j)", a=4, s=2, p=P, t=4)
-    nz_rows = nz.rearrange("o e (g l) i -> (o e g) (l i)", g=8)
+    nz_rows = nz.rearrange("o e (g l) i -> (o e g) (l i)", g=PASSES)
     x_rows = x.rearrange("o c (q r) w -> (o c) r q w", q=4, r=P)
-    out_0_rows = out_0.rearrange("o c (jh kh a r) w -> kh (o c jh) a (r w)", jh=16, kh=8, a=2, r=2)
-    out_1_rows = out_1.rearrange("o e (g p t) j -> (o e g) p (t j)", g=8, p=P, t=4)
+    x_row_pairs = x.rearrange("o c (q r a) w -> (o c) r q (a w)", q=2, r=P, a=2)
+    out_0_rows = out_0.rearrange("o c (jh kh a) w -> kh (o c jh) (a w)", jh=16, kh=8, a=4)
+    out_1_rows = out_1.rearrange("o e (g p t) j -> (o e g) p (t j)", g=PASSES, p=P, t=4)
 
     with ExitStack() as ctx:
         keep = ctx.enter_context(tc.tile_pool(name="keep", bufs=1))
@@ -35,8 +40,8 @@ def tile_decode_atten_v_kernel(tc, x, attentions, nz, grad_out, out_0, out_1):
         psum = ctx.enter_context(tc.psum_pool(name="psum", bufs=1))
         ctx.enter_context(tc.manual_schedule())
 
-        def bank(i):
-            return psum.tile([P, 512], F32, name="bank%d" % i, tag="bank%d" % i)
+        def bank(b):
+            return psum.tile([P, 512], F32, name="bank%d" % b, tag="bank%d" % b)
 
         def copy(engine, out, in_):
             if engine == "scalar":
@@ -54,7 +59,7 @@ def tile_decode_atten_v_kernel(tc, x, attentions, nz, grad_out, out_0, out_1):
         nc.vector.memset(nz_sb[:], 0.0)
         grad_sb, att_sb, x_sb = {}, {}, {}
 
-        def load_grad(h, s, first, last):
+        def load_grad(h, s, first=0, last=8):
             if first == 0:
                 grad_sb[h, s] = keep.tile([P, 8, 512], BF16, name="grad_sb%d%d" % (h, s))
             for m in range(first, last):
@@ -64,35 +69,39 @@ def tile_decode_atten_v_kernel(tc, x, attentions, nz, grad_out, out_0, out_1):
             att_sb[s, n] = keep.tile([P, 2, 1024], BF16, name="att_sb%d%d" % (s, n))
             nc.sync.dma_start(out=att_sb[s, n][:], in_=att_rows[s][:, 2 * n:2 * n + 2, :])
 
-
         def load_x(c):
-            x_sb[c] = work.tile([P, 4, 512], BF16, name="x_sb", tag="x_then_da", bufs=8)
-            nc.sync.dma_start(out=x_sb[c][:], in_=x_rows[c])
+            rows = x_row_pairs[c] if c >= FIRST_PAIRED else x_rows[c]
+            x_sb[c] = work.tile(rows.shape, BF16, name="x_sb", tag="x_then_da", bufs=CHANNELS)
+            nc.sync.dma_start(out=x_sb[c][:], in_=rows)
 
-        load_grad(0, 0, 0, 8)
-        nc.sync.dma_start(out=nz_sb[0:8, :], in_=nz_rows)
+        load_grad(0, 0, last=1)
+        nc.sync.dma_start(out=nz_sb[0:PASSES, :], in_=nz_rows)
+        load_grad(0, 0, first=1)
         load_att(0, 0)
-        load_grad(0, 1, 0, 8)
+        load_grad(0, 1)
         load_att(0, 1)
         load_att(1, 0)
         load_x(0)
-        load_grad(1, 0, 0, 8)
-        load_att(1, 1)
+        load_grad(1, 0)
         load_x(1)
+        load_att(1, 1)
         load_x(2)
-        load_grad(1, 1, 0, 8)
-        for c in range(3, 8):
+        load_x(3)
+        load_grad(1, 1)
+        for c in range(4, CHANNELS):
             load_x(c)
 
         ident = keep.tile([P, P], F32, name="ident")
         make_identity(nc, ident[:])
-        dz_l_codes = keep.tile([P, (2 * SLOTS + 1) * 256], U32, name="dz_l_codes", align_bytes=64)
-        dz_l_scales = keep.tile([P, (2 * SLOTS + 1) * 256], U8, name="dz_l_scales", align_bytes=64)
-        u_codes = keep.tile([P, 768], U32, name="u_codes", align_bytes=64)
-        u_scales = keep.tile([P, 768], U8, name="u_scales", align_bytes=64)
+
+        dz_l_codes = keep.tile([P, 9 * HALF_BANK], U32, name="dz_l_codes", align_bytes=64)
+        dz_l_scales = keep.tile([P, 9 * HALF_BANK], U8, name="dz_l_scales", align_bytes=64)
+        u_codes = keep.tile([P, 3 * HALF_BANK], U32, name="u_codes", align_bytes=64)
+        u_scales = keep.tile([P, 3 * HALF_BANK], U8, name="u_scales", align_bytes=64)
         for codes, scales in ((dz_l_codes, dz_l_scales), (u_codes, u_scales)):
-            nc.vector.memset(codes[:].rearrange("p (n w) -> p n w", w=256)[:, 0::2, :], 0)
-            nc.vector.memset(scales[:].bitcast(U32).rearrange("p (n w) -> p n w", w=64)[:, 0::2, :], 0)
+            nc.vector.memset(codes[:].rearrange("p (n w) -> p n w", w=HALF_BANK)[:, 0::2, :], 0)
+            nc.vector.memset(scales[:].bitcast(U32).rearrange("p (n w) -> p n w", w=HALF_BANK // 4)[:, 0::2, :], 0)
+
         sum4 = keep.tile([P, 32], F32, name="sum4")
         nc.vector.tensor_reduce(out=sum4[:], in_=ident[:].rearrange("p (r a) -> p r a", a=4),
                                 axis=mybir.AxisListType.X, op=ALU.add)
@@ -104,15 +113,22 @@ def tile_decode_atten_v_kernel(tc, x, attentions, nz, grad_out, out_0, out_1):
                               in_=ident[:].rearrange("p (b q v r) -> p q r v b", b=4, q=4, v=2))
         pool_rows = keep.tile([P, 32], BF16, name="pool_rows")
         times("scalar", pool_rows[:].rearrange("p (kh r) -> p kh r", r=4),
-              sum4[:].rearrange("p (r kh) -> p kh r", r=4), 0.0625)
-        inv_nz = keep.tile([P, 32], F32, name="inv_nz")
+              sum4[:].rearrange("p (r kh) -> p kh r", r=4), MEAN_16)
+        sum2 = keep.tile([P, 64], F32, name="sum2")
+        nc.vector.tensor_reduce(out=sum2[:], in_=ident[:].rearrange("p (r a) -> p r a", a=2),
+                                axis=mybir.AxisListType.X, op=ALU.add)
+        pool_pairs = keep.tile([P, 64], BF16, name="pool_pairs")
+        times("scalar", pool_pairs[:].rearrange("p (kh r) -> p kh r", r=8),
+              sum2[:].rearrange("p (r kh) -> p kh r", r=8), MEAN_16)
+
+        inv_nz = keep.tile([P, 4 * PASSES], F32, name="inv_nz")
         nz_flipped = bank(1)
         for t in range(4):
             nc.tensor.transpose(nz_flipped[:, t * P:(t + 1) * P], nz_sb[:, t:512:4], ident[:])
         nc.vector.reciprocal(out=inv_nz[:].rearrange("p (g t) -> p t g", t=4),
-                             in_=nz_flipped[:].rearrange("p (t g) -> p t g", t=4)[:, :, 0:8])
+                             in_=nz_flipped[:].rearrange("p (t g) -> p t g", t=4)[:, :, 0:PASSES])
 
-        dz = [keep.tile([P, 4, 2, 2, 128], BF16, name="dz%d" % g) for g in range(8)]
+        dz = [keep.tile([P, 4, 2, 2, 128], BF16, name="dz%d" % g) for g in range(PASSES)]
         att_codes = [keep.tile([P, 1024], U32, name="att_codes%d" % s, align_bytes=64) for s in range(2)]
         att_scales = [keep.tile([P, 1024], U8, name="att_scales%d" % s, align_bytes=64) for s in range(2)]
         live = {}
@@ -120,8 +136,8 @@ def tile_decode_atten_v_kernel(tc, x, attentions, nz, grad_out, out_0, out_1):
         def sort_grad(h, s, t):
             sorted_words = work.tile([P, 4, P], F32, name="sorted_words", bufs=6)
             words = grad_sb[h, s][:].rearrange("p m w -> p (m w)").bitcast(F32)
-            nc.scalar.copy(out=sorted_words[:].rearrange("p w (mh ml) -> p mh w ml", ml=4),
-                           in_=words.rearrange("p (mh ml t w) -> p t mh w ml", ml=4, t=4, w=4)[:, t])
+            nc.scalar.copy(out=sorted_words[:].rearrange("p w (hi lo) -> p hi w lo", lo=4),
+                           in_=words.rearrange("p (hi lo t w) -> p t hi w lo", lo=4, t=4, w=4)[:, t])
             live["sorted", h, s, t] = sorted_words
 
         def flip_grad(h, s, t, b):
@@ -134,10 +150,10 @@ def tile_decode_atten_v_kernel(tc, x, attentions, nz, grad_out, out_0, out_1):
 
         def divide(h, s, t, engine):
             values = live["flipped", h, s, t][:].bitcast(BF16).rearrange(
-                "p (w0 w1 c a ke) -> p a w1 c w0 ke", w0=2, w1=2, c=8, a=4)
+                "p (w0 w1 c a ke) -> p a w1 c w0 ke", w0=2, w1=2, c=CHANNELS, a=4)
             for a in range(4):
                 g = 2 * a + s
-                times(engine, dz[g][:, t, :, h, :].rearrange("p w1 (c w0 ke) -> p w1 c w0 ke", c=8, w0=2),
+                times(engine, dz[g][:, t, :, h, :].rearrange("p w1 (c w0 ke) -> p w1 c w0 ke", c=CHANNELS, w0=2),
                       values[:, a], inv_nz[:, 4 * g + t:4 * g + t + 1])
 
         def weave_dz(h, s, a, engine):
@@ -147,8 +163,8 @@ def tile_decode_atten_v_kernel(tc, x, attentions, nz, grad_out, out_0, out_1):
             live["woven_dz", h, s, a] = woven
 
         def quantize_dz_l(h, s, a):
-            at = (2 * a + 1) * 256
-            nc.vector.quantize_mx(out=dz_l_codes[:, at:at + 256].bitcast(E5M2X4), scales=dz_l_scales[:, at:at + 256],
+            real = slice((2 * a + 1) * HALF_BANK, (2 * a + 2) * HALF_BANK)
+            nc.vector.quantize_mx(out=dz_l_codes[:, real].bitcast(E5M2X4), scales=dz_l_scales[:, real],
                                   in_=live["woven_dz", h, s, a][:])
 
         def weave_att(s, a):
@@ -158,25 +174,26 @@ def tile_decode_atten_v_kernel(tc, x, attentions, nz, grad_out, out_0, out_1):
             live["woven_att", s, a] = woven
 
         def quantize_att(s, a):
-            nc.vector.quantize_mx(out=att_codes[s][:, a * 256:(a + 1) * 256].bitcast(E4M3X4),
-                                  scales=att_scales[s][:, a * 256:(a + 1) * 256], in_=live["woven_att", s, a][:])
+            columns = slice(a * 256, (a + 1) * 256)
+            nc.vector.quantize_mx(out=att_codes[s][:, columns].bitcast(E4M3X4), scales=att_scales[s][:, columns],
+                                  in_=live["woven_att", s, a][:])
 
         def multiply_l(h, s, a):
             if s == 0 and a == 0:
                 live["du", h] = bank(h)
             for half in range(2):
                 js = slice(a * 256 + half * P, a * 256 + (half + 1) * P)
-                at = (2 * a + 1 - half) * 256
+                window = slice((2 * a + 1 - half) * HALF_BANK, (2 * a + 3 - half) * HALF_BANK)
                 nc.tensor.matmul_mx(out=live["du", h][:], lhsT=att_codes[s][:, js].bitcast(E4M3X4),
-                                    lhsT_scale=att_scales[s][:, js],
-                                    rhs=dz_l_codes[:, at:at + 512].bitcast(E5M2X4), rhs_scale=dz_l_scales[:, at:at + 512],
+                                    lhsT_scale=att_scales[s][:, js], rhs=dz_l_codes[:, window].bitcast(E5M2X4),
+                                    rhs_scale=dz_l_scales[:, window],
                                     start=(s == 0 and a == 0 and half == 0), stop=(s == 1 and a == 3 and half == 1))
 
         def copy_du(h):
-            du_sb = work.tile([P, 2, 256], F32, name="du_sb", bufs=1)
+            du_sb = work.tile([P, 2, HALF_BANK], F32, name="du_sb", bufs=1)
             for half in range(2):
                 nc.scalar.copy(out=du_sb[:, half, :].rearrange("p (c0 c21 w1 r) -> p c0 c21 w1 r", c0=2, c21=4, w1=2),
-                               in_=live["du", h][:, half * 256:(half + 1) * 256].rearrange(
+                               in_=live["du", h][:, half * HALF_BANK:(half + 1) * HALF_BANK].rearrange(
                                    "p (w1 c21 c0 r) -> p c0 c21 w1 r", w1=2, c21=4, c0=2))
             live["du_sb", h] = du_sb
 
@@ -194,25 +211,32 @@ def tile_decode_atten_v_kernel(tc, x, attentions, nz, grad_out, out_0, out_1):
             nc.vector.transpose(out=du_rows[:], in_=live["du_flipped", h][:])
             live["du_rows", h] = du_rows
 
-        def spread_du(h, k, engine):
+        def spread_du(h, k, engines):
             spread = work.tile([P, 2, 512], F32, name="spread", bufs=5)
             values = live["du_rows", h][:].rearrange("p (pair k e) -> p k pair e", k=4, e=2)[:, k]
-            for row in range(2):
-                times(engine[row], spread[:, row, :].rearrange("p (pair e b) -> p pair e b", e=2, b=4),
-                      values.unsqueeze(3).to_broadcast([P, 64, 2, 4]), 0.0625)
-            nc.sync.dma_start(out=out_0_rows[4 * h + k],
-                              in_=spread[:].rearrange("p r w -> p (r w)").unsqueeze(1).to_broadcast([P, 2, 1024]))
+            rows = len(engines)
+            for row in range(rows):
+                times(engines[row], spread[:, row, :].rearrange("p (pair e b) -> p pair e b", e=2, b=4),
+                      values.unsqueeze(3).to_broadcast([P, 64, 2, 4]), MEAN_16)
+            written = spread[:].rearrange("p r w -> p (r w)")[:, 0:rows * 512]
+            nc.sync.dma_start(out=out_0_rows[4 * h + k].rearrange("p (n w) -> p n w", w=rows * 512),
+                              in_=written.unsqueeze(1).to_broadcast([P, 4 // rows, rows * 512]))
 
         def pool_x(c):
             if c % 2 == 0:
-                live["pooled", c // 2] = bank(4 + c // 2)
-            sums = live["pooled", c // 2][:].rearrange("p (c kh q v r) -> p c q v kh r", c=2, kh=8, q=4, v=2)
-            for q in range(4):
+                live["pooled", c // 2] = bank(FIRST_POOL_BANK + c // 2)
+            rows_held = 2 if c >= FIRST_PAIRED else 1
+            matrix = pool_pairs if c >= FIRST_PAIRED else pool_rows
+            sums = live["pooled", c // 2][:].rearrange("p (c kh q j v r) -> p c q v kh j r",
+                                                       c=2, kh=8, j=rows_held, v=2, r=4)
+            for q in range(4 // rows_held):
                 for v in range(2):
-                    for b0 in range(2):
-                        nc.tensor.matmul(sums[:, c % 2, q, v], lhsT=x_sb[c][:, q, v * 256 + b0:(v + 1) * 256:2],
-                                         rhs=pool_rows[:].rearrange("p (kh r) -> p kh r", r=4),
-                                         start=(b0 == 0), stop=(b0 == 1))
+                    for n in range(2 * rows_held):
+                        row, b0 = divmod(n, 2)
+                        at = row * 512 + v * 256
+                        nc.tensor.matmul(sums[:, c % 2, q, v], lhsT=x_sb[c][:, q, at + b0:at + 256:2],
+                                         rhs=matrix[:].rearrange("p (kh j r) -> p kh j r", j=rows_held, r=4),
+                                         start=(n == 0), stop=(n == 2 * rows_held - 1))
 
         pair_sums = keep.tile([P, 2048], F32, name="pair_sums", align_bytes=64)
         u_bf = keep.tile([P, 1024], BF16, name="u_bf")
@@ -221,24 +245,26 @@ def tile_decode_atten_v_kernel(tc, x, attentions, nz, grad_out, out_0, out_1):
             nc.vector.transpose(out=pair_sums[:, n * 512:(n + 1) * 512], in_=live["pooled", n][:])
 
         def add_pooled():
-            pairs = pair_sums[:].rearrange("p (c h k v w0 e b) -> p v w0 b c h k e", c=8, h=2, k=4, v=4, w0=2, e=2)
-            result = u_bf[:].rearrange("p (v h c w0 k e) -> p v w0 c h k e", v=4, h=2, c=8, w0=2, k=4)
-            for v in range(4):
+            pairs = pair_sums[:].rearrange("p (c h k z w0 e b) -> p z w0 b c h k e",
+                                           c=CHANNELS, h=2, k=4, z=4, w0=2, e=2)
+            result = u_bf[:].rearrange("p (z h c w0 k e) -> p z w0 c h k e", z=4, h=2, c=CHANNELS, w0=2, k=4)
+            for z in range(4):
                 for w0 in range(2):
-                    nc.vector.tensor_tensor(out=result[:, v, w0], in0=pairs[:, v, w0, 0], in1=pairs[:, v, w0, 1],
+                    nc.vector.tensor_tensor(out=result[:, z, w0], in0=pairs[:, z, w0, 0], in1=pairs[:, z, w0, 1],
                                             op=ALU.add)
 
-        def flip_u(b):
+        def flip_and_weave_u(b):
             flipped = bank(b)
-            for v in range(4):
-                nc.tensor.transpose(flipped[:, v * P:(v + 1) * P], u_bf[:].bitcast(F32)[:, v * P:(v + 1) * P], perm_u[:])
+            for z in range(4):
+                nc.tensor.transpose(flipped[:, z * P:(z + 1) * P], u_bf[:].bitcast(F32)[:, z * P:(z + 1) * P], perm_u[:])
             woven = keep.tile([P, 1024], BF16, name="woven_u", align_bytes=64)
-            nc.scalar.copy(out=woven[:].bitcast(F32).rearrange("p (j v) -> p j v", v=4),
-                           in_=flipped[:].rearrange("p (v j) -> p j v", v=4))
+            nc.scalar.copy(out=woven[:].bitcast(F32).rearrange("p (j z) -> p j z", z=4),
+                           in_=flipped[:].rearrange("p (z j) -> p j z", z=4))
             live["woven_u"] = woven
 
         def quantize_u():
-            nc.vector.quantize_mx(out=u_codes[:, 256:512].bitcast(E4M3X4), scales=u_scales[:, 256:512],
+            real = slice(HALF_BANK, 2 * HALF_BANK)
+            nc.vector.quantize_mx(out=u_codes[:, real].bitcast(E4M3X4), scales=u_scales[:, real],
                                   in_=live["woven_u"][:])
 
         def flip_dz(g, pair, b):
@@ -267,46 +293,49 @@ def tile_decode_atten_v_kernel(tc, x, attentions, nz, grad_out, out_0, out_1):
             sums = bank(b)
             for half in range(2):
                 ls = slice((2 * pair + half) * P, (2 * pair + half + 1) * P)
-                at = (1 - half) * 256
+                window = slice((1 - half) * HALF_BANK, (3 - half) * HALF_BANK)
                 nc.tensor.matmul_mx(out=sums[:], lhsT=codes[:, ls].bitcast(E5M2X4), lhsT_scale=scales[:, ls],
-                                    rhs=u_codes[:, at:at + 512].bitcast(E4M3X4), rhs_scale=u_scales[:, at:at + 512],
+                                    rhs=u_codes[:, window].bitcast(E4M3X4), rhs_scale=u_scales[:, window],
                                     start=(half == 0), stop=(half == 1))
             live["da", g, pair] = sums
 
         def copy_da(g, pair, engine):
             if pair == 0:
-                live["da_sb", g] = work.tile([P, 1024], F32, name="da_sb", tag="x_then_da", bufs=8)
+                live["da_sb", g] = work.tile([P, 1024], F32, name="da_sb", tag="x_then_da", bufs=CHANNELS)
             copy(engine, live["da_sb", g][:, pair * 512:(pair + 1) * 512], live["da", g, pair][:])
             if pair == 1:
                 nc.sync.dma_start(out=out_1_rows[g], in_=live["da_sb", g][:])
 
-        both = ("scalar", "vector")
-        units = ((0, 0), (0, 1), (1, 0))
-        flip_banks = ((4, 5, 6, 7), (1, 2, 3, 1), (2, 3, 1, 2))
+        one_row, two_rows, two_rows_shared = ("scalar",), ("scalar", "scalar"), ("scalar", "vector")
+
         for t in range(4):
             sort_grad(0, 0, t)
-            flip_grad(0, 0, t, flip_banks[0][t])
+            flip_grad(0, 0, t, FIRST_POOL_BANK + t)
             divide(0, 0, t, "vector")
         weave_att(0, 0)
         weave_dz(0, 0, 0, "vector")
+
+        pool_steps = (2, 4, 5, 6)
         for step in range(8):
             s, i = divmod(step, 4)
-            sort_grad(*units[s + 1], i)
+            following = ((0, 1), (1, 0))[s]
+            sort_grad(*following, i)
             if step < 7:
                 weave_att(*divmod(step + 1, 4))
-            flip_grad(*units[s + 1], i, flip_banks[s + 1][i])
+            flip_grad(*following, i, 1 + step % 3)
             if step > 0:
                 multiply_l(0, *divmod(step - 1, 4))
-            if step in (2, 5, 6):
-                pool_x((2, 5, 6).index(step))
+            if step in pool_steps:
+                pool_x(pool_steps.index(step))
             if i < 3:
                 weave_dz(0, s, i + 1, "vector")
             quantize_dz_l(0, s, i)
             quantize_att(s, i)
-            divide(*units[s + 1], i, "vector")
+            divide(*following, i, "vector")
             if i == 3:
-                weave_dz(*units[s + 1], 0, "vector")
+                weave_dz(*following, 0, "vector")
         multiply_l(0, 1, 3)
+
         sort_grad(1, 1, 0)
         sort_grad(1, 1, 1)
         copy_du(0)
@@ -316,17 +345,18 @@ def tile_decode_atten_v_kernel(tc, x, attentions, nz, grad_out, out_0, out_1):
         flip_grad(1, 1, 1, 7)
         flip_du(0, 0)
         flip_grad(1, 1, 2, 2)
-        pool_x(3)
+        pool_x(4)
         weave_dz(1, 0, 1, "vector")
         quantize_dz_l(1, 0, 0)
-        divide(1, 1, 0, "vector")
         swap_du(0)
+        divide(1, 1, 0, "vector")
         flip_grad(1, 1, 3, 3)
+
         for i in range(1, 4):
-            spread_du(0, i - 1, both)
+            spread_du(0, i - 1, one_row)
             multiply_l(1, 0, i - 1)
-            if i > 1:
-                pool_x(2 + i)
+            if i == 2:
+                pool_x(5)
             if i < 3:
                 weave_dz(1, 0, i + 1, "vector")
                 divide(1, 1, i, "scalar")
@@ -334,54 +364,63 @@ def tile_decode_atten_v_kernel(tc, x, attentions, nz, grad_out, out_0, out_1):
                 divide(1, 1, 3, "vector")
             quantize_dz_l(1, 0, i)
         multiply_l(1, 0, 3)
+
+        flip_dz(0, 0, 0)
+        flip_dz(0, 1, 2)
         weave_dz(1, 1, 0, "vector")
         weave_dz(1, 1, 3, "scalar")
-        spread_du(0, 3, ("scalar", "scalar"))
+        spread_du(0, 3, one_row)
+        weave_dz_n(0, 0, "scalar")
+        weave_dz_n(0, 1, "scalar")
         for i in range(4):
             if i < 2:
                 weave_dz(1, 1, i + 1, "vector")
             quantize_dz_l(1, 1, i)
             multiply_l(1, 1, i)
+
         copy_du(1)
         pool_x(6)
-        swap_pooled(0)
-        swap_pooled(1)
-        swap_pooled(2)
-        flip_du(1, 3)
-        pool_x(7)
-        flip_dz(0, 0, 0)
-        flip_dz(0, 1, 2)
-        flip_dz(1, 0, 4)
-        flip_dz(1, 1, 5)
-        swap_du(1)
-        spread_du(1, 0, both)
-        swap_pooled(3)
-        weave_dz_n(0, 0, "scalar")
-        spread_du(1, 1, both)
-        add_pooled()
-        weave_dz_n(0, 1, "scalar")
-        flip_dz(2, 0, 1)
-        flip_dz(2, 1, 6)
-        flip_u(0)
-        weave_dz_n(1, 0, "vector")
+        for n in range(3):
+            swap_pooled(n)
         quantize_dz_n(0)
-        quantize_u()
-        weave_dz_n(1, 1, "scalar")
-        weave_dz_n(2, 0, "vector")
+        flip_du(1, 0)
+        pool_x(7)
+        flip_dz(2, 0, 3)
+        flip_dz(2, 1, 2)
+        swap_du(1)
+        spread_du(1, 0, two_rows_shared)
+        swap_pooled(3)
+        weave_dz_n(2, 0, "scalar")
         weave_dz_n(2, 1, "scalar")
-        quantize_dz_n(1)
-        for g in range(8):
-            multiply_n(g, 0, (0, 3)[g % 2])
-            multiply_n(g, 1, (2, 1)[g % 2])
-            if g + 3 < 8:
-                flip_dz(g + 3, 0, 4 + (2 * g + 3) % 4)
-                flip_dz(g + 3, 1, 4 + (2 * g) % 4)
-            if g < 2:
-                spread_du(1, 2 + g, both)
-            if g + 2 < 8:
-                quantize_dz_n(g + 2)
+        flip_dz(4, 0, 3)
+        flip_dz(4, 1, 1)
+        spread_du(1, 1, two_rows)
+        add_pooled()
+        flip_dz(6, 0, 4)
+        flip_dz(6, 1, 5)
+        flip_and_weave_u(6)
+        quantize_dz_n(2)
+        weave_dz_n(4, 0, "vector")
+        quantize_u()
+        weave_dz_n(4, 1, "scalar")
+        spread_du(1, 2, two_rows_shared)
+        weave_dz_n(6, 0, "vector")
+        weave_dz_n(6, 1, "scalar")
+        quantize_dz_n(4)
+
+        order = (0, 2, 4, 6, 1, 3, 5, 7)
+        for n, g in enumerate(order):
+            multiply_n(g, 0, 2 * (n % 2))
+            multiply_n(g, 1, 2 * (n % 2) + 1)
+            if n + 4 < PASSES:
+                flip_dz(order[n + 4], 0, 4 + (2 * n + 3) % 4)
+                flip_dz(order[n + 4], 1, 4 + (2 * n) % 4)
+            if n == 0:
+                spread_du(1, 3, two_rows_shared)
+            if n + 3 < PASSES:
+                quantize_dz_n(order[n + 3])
             copy_da(g, 0, "scalar")
             copy_da(g, 1, "vector")
-            if g + 3 < 8:
-                weave_dz_n(g + 3, 0, "scalar")
-                weave_dz_n(g + 3, 1, "vector" if g % 2 == 0 else "scalar")
+            if n + 4 < PASSES:
+                weave_dz_n(order[n + 4], 0, "scalar")
+                weave_dz_n(order[n + 4], 1, "vector" if n % 2 == 0 else "scalar")

from contextlib import ExitStack

import concourse.mybir as mybir
from concourse.masks import make_identity

F32 = mybir.dt.float32
BF16 = mybir.dt.bfloat16
U32 = mybir.dt.uint32
U8 = mybir.dt.uint8
E4M3X4 = mybir.dt.float8_e4m3fn_x4
E5M2X4 = mybir.dt.float8_e5m2_x4
ALU = mybir.AluOpType
ACT = mybir.ActivationFunctionType

FLOPS = 2 * 2 * 4096 * 256 * 512

P = 128
CHANNELS = 8
PASSES = 8
HALF_BANK = 256
MEAN_16 = 0.0625
FIRST_PAIRED = 4
FIRST_POOL_BANK = 4


def tile_decode_atten_v_kernel(tc, x, attentions, nz, grad_out, out_0, out_1):
    nc = tc.nc

    grad_rows = grad_out.rearrange("o c (a s m h k) w -> s h m (o c a) k w", a=4, s=2, m=8, h=2, k=4)
    att_rows = attentions.rearrange("o e (a s p t) j -> s p (o e a) (t j)", a=4, s=2, p=P, t=4)
    nz_rows = nz.rearrange("o e (g l) i -> (o e g) (l i)", g=PASSES)
    x_rows = x.rearrange("o c (q r) w -> (o c) r q w", q=4, r=P)
    x_row_pairs = x.rearrange("o c (q r a) w -> (o c) r q (a w)", q=2, r=P, a=2)
    out_0_rows = out_0.rearrange("o c (jh kh a) w -> kh (o c jh) (a w)", jh=16, kh=8, a=4)
    out_1_rows = out_1.rearrange("o e (g p t) j -> (o e g) p (t j)", g=PASSES, p=P, t=4)

    with ExitStack() as ctx:
        keep = ctx.enter_context(tc.tile_pool(name="keep", bufs=1))
        work = ctx.enter_context(tc.tile_pool(name="work", bufs=1))
        psum = ctx.enter_context(tc.psum_pool(name="psum", bufs=1))
        ctx.enter_context(tc.manual_schedule())

        def bank(b):
            return psum.tile([P, 512], F32, name="bank%d" % b, tag="bank%d" % b)

        def copy(engine, out, in_):
            if engine == "scalar":
                nc.scalar.copy(out=out, in_=in_)
            else:
                nc.vector.tensor_copy(out=out, in_=in_)

        def times(engine, out, in_, factor):
            if engine == "scalar":
                nc.scalar.activation(out=out, in_=in_, func=ACT.Copy, scale=factor)
            else:
                nc.vector.tensor_scalar(out=out, in0=in_, scalar1=factor, scalar2=None, op0=ALU.mult)

        nz_sb = keep.tile([P, 512], F32, name="nz_sb")
        nc.vector.memset(nz_sb[:], 0.0)
        grad_sb, att_sb, x_sb = {}, {}, {}

        def load_grad(h, s, first=0, last=8):
            if first == 0:
                grad_sb[h, s] = keep.tile([P, 8, 512], BF16, name="grad_sb%d%d" % (h, s))
            for m in range(first, last):
                nc.sync.dma_start(out=grad_sb[h, s][:, m, :], in_=grad_rows[s, h, m])

        def load_att(s, n):
            att_sb[s, n] = keep.tile([P, 2, 1024], BF16, name="att_sb%d%d" % (s, n))
            nc.sync.dma_start(out=att_sb[s, n][:], in_=att_rows[s][:, 2 * n:2 * n + 2, :])

        def load_x(c):
            rows = x_row_pairs[c] if c >= FIRST_PAIRED else x_rows[c]
            x_sb[c] = work.tile(rows.shape, BF16, name="x_sb", tag="x_then_da", bufs=CHANNELS)
            nc.sync.dma_start(out=x_sb[c][:], in_=rows)

        load_grad(0, 0, last=1)
        nc.sync.dma_start(out=nz_sb[0:PASSES, :], in_=nz_rows)
        load_grad(0, 0, first=1)
        load_att(0, 0)
        load_grad(0, 1)
        load_att(0, 1)
        load_att(1, 0)
        load_x(0)
        load_grad(1, 0)
        load_x(1)
        load_att(1, 1)
        load_x(2)
        load_x(3)
        load_grad(1, 1)
        for c in range(4, CHANNELS):
            load_x(c)

        ident = keep.tile([P, P], F32, name="ident")
        make_identity(nc, ident[:])

        dz_l_codes = keep.tile([P, 9 * HALF_BANK], U32, name="dz_l_codes", align_bytes=64)
        dz_l_scales = keep.tile([P, 9 * HALF_BANK], U8, name="dz_l_scales", align_bytes=64)
        u_codes = keep.tile([P, 3 * HALF_BANK], U32, name="u_codes", align_bytes=64)
        u_scales = keep.tile([P, 3 * HALF_BANK], U8, name="u_scales", align_bytes=64)
        for codes, scales in ((dz_l_codes, dz_l_scales), (u_codes, u_scales)):
            nc.vector.memset(codes[:].rearrange("p (n w) -> p n w", w=HALF_BANK)[:, 0::2, :], 0)
            nc.vector.memset(scales[:].bitcast(U32).rearrange("p (n w) -> p n w", w=HALF_BANK // 4)[:, 0::2, :], 0)

        sum4 = keep.tile([P, 32], F32, name="sum4")
        nc.vector.tensor_reduce(out=sum4[:], in_=ident[:].rearrange("p (r a) -> p r a", a=4),
                                axis=mybir.AxisListType.X, op=ALU.add)
        perm_du = keep.tile([P, P], F32, name="perm_du")
        nc.vector.tensor_copy(out=perm_du[:].rearrange("p (jw jh) -> p jw jh", jw=16),
                              in_=ident[:].rearrange("p (jh jw) -> p jw jh", jw=16))
        perm_u = keep.tile([P, P], F32, name="perm_u")
        nc.vector.tensor_copy(out=perm_u[:].rearrange("p (q r v b) -> p q r v b", q=4, r=4, v=2),
                              in_=ident[:].rearrange("p (b q v r) -> p q r v b", b=4, q=4, v=2))
        pool_rows = keep.tile([P, 32], BF16, name="pool_rows")
        times("scalar", pool_rows[:].rearrange("p (kh r) -> p kh r", r=4),
              sum4[:].rearrange("p (r kh) -> p kh r", r=4), MEAN_16)
        sum2 = keep.tile([P, 64], F32, name="sum2")
        nc.vector.tensor_reduce(out=sum2[:], in_=ident[:].rearrange("p (r a) -> p r a", a=2),
                                axis=mybir.AxisListType.X, op=ALU.add)
        pool_pairs = keep.tile([P, 64], BF16, name="pool_pairs")
        times("scalar", pool_pairs[:].rearrange("p (kh r) -> p kh r", r=8),
              sum2[:].rearrange("p (r kh) -> p kh r", r=8), MEAN_16)

        inv_nz = keep.tile([P, 4 * PASSES], F32, name="inv_nz")
        nz_flipped = bank(1)
        for t in range(4):
            nc.tensor.transpose(nz_flipped[:, t * P:(t + 1) * P], nz_sb[:, t:512:4], ident[:])
        nc.vector.reciprocal(out=inv_nz[:].rearrange("p (g t) -> p t g", t=4),
                             in_=nz_flipped[:].rearrange("p (t g) -> p t g", t=4)[:, :, 0:PASSES])

        dz = [keep.tile([P, 4, 2, 2, 128], BF16, name="dz%d" % g) for g in range(PASSES)]
        att_codes = [keep.tile([P, 1024], U32, name="att_codes%d" % s, align_bytes=64) for s in range(2)]
        att_scales = [keep.tile([P, 1024], U8, name="att_scales%d" % s, align_bytes=64) for s in range(2)]
        live = {}

        def sort_grad(h, s, t):
            sorted_words = work.tile([P, 4, P], F32, name="sorted_words", bufs=6)
            words = grad_sb[h, s][:].rearrange("p m w -> p (m w)").bitcast(F32)
            nc.scalar.copy(out=sorted_words[:].rearrange("p w (hi lo) -> p hi w lo", lo=4),
                           in_=words.rearrange("p (hi lo t w) -> p t hi w lo", lo=4, t=4, w=4)[:, t])
            live["sorted", h, s, t] = sorted_words

        def flip_grad(h, s, t, b):
            flipped = bank(b)
            for w1 in range(2):
                for w0 in range(2):
                    at = (2 * w0 + w1) * P
                    nc.tensor.transpose(flipped[:, at:at + P], live["sorted", h, s, t][:, 2 * w1 + w0, :], ident[:])
            live["flipped", h, s, t] = flipped

        def divide(h, s, t, engine):
            values = live["flipped", h, s, t][:].bitcast(BF16).rearrange(
                "p (w0 w1 c a ke) -> p a w1 c w0 ke", w0=2, w1=2, c=CHANNELS, a=4)
            for a in range(4):
                g = 2 * a + s
                times(engine, dz[g][:, t, :, h, :].rearrange("p w1 (c w0 ke) -> p w1 c w0 ke", c=CHANNELS, w0=2),
                      values[:, a], inv_nz[:, 4 * g + t:4 * g + t + 1])

        def weave_dz(h, s, a, engine):
            woven = work.tile([P, 1024], BF16, name="woven_dz", bufs=4, align_bytes=64)
            copy(engine, woven[:].rearrange("p (w1 n t) -> p w1 n t", w1=2, t=4),
                 dz[2 * a + s][:, :, :, h, :].rearrange("p t w1 n -> p w1 n t"))
            live["woven_dz", h, s, a] = woven

        def quantize_dz_l(h, s, a):
            real = slice((2 * a + 1) * HALF_BANK, (2 * a + 2) * HALF_BANK)
            nc.vector.quantize_mx(out=dz_l_codes[:, real].bitcast(E5M2X4), scales=dz_l_scales[:, real],
                                  in_=live["woven_dz", h, s, a][:])

        def weave_att(s, a):
            woven = work.tile([P, 1024], BF16, name="woven_att", bufs=4, align_bytes=64)
            nc.scalar.copy(out=woven[:].rearrange("p (j t) -> p j t", t=4),
                           in_=att_sb[s, a // 2][:, a % 2, :].rearrange("p (t j) -> p j t", t=4))
            live["woven_att", s, a] = woven

        def quantize_att(s, a):
            columns = slice(a * 256, (a + 1) * 256)
            nc.vector.quantize_mx(out=att_codes[s][:, columns].bitcast(E4M3X4), scales=att_scales[s][:, columns],
                                  in_=live["woven_att", s, a][:])

        def multiply_l(h, s, a):
            if s == 0 and a == 0:
                live["du", h] = bank(h)
            for half in range(2):
                js = slice(a * 256 + half * P, a * 256 + (half + 1) * P)
                window = slice((2 * a + 1 - half) * HALF_BANK, (2 * a + 3 - half) * HALF_BANK)
                nc.tensor.matmul_mx(out=live["du", h][:], lhsT=att_codes[s][:, js].bitcast(E4M3X4),
                                    lhsT_scale=att_scales[s][:, js], rhs=dz_l_codes[:, window].bitcast(E5M2X4),
                                    rhs_scale=dz_l_scales[:, window],
                                    start=(s == 0 and a == 0 and half == 0), stop=(s == 1 and a == 3 and half == 1))

        def copy_du(h):
            du_sb = work.tile([P, 2, HALF_BANK], F32, name="du_sb", bufs=1)
            for half in range(2):
                nc.scalar.copy(out=du_sb[:, half, :].rearrange("p (c0 c21 w1 r) -> p c0 c21 w1 r", c0=2, c21=4, w1=2),
                               in_=live["du", h][:, half * HALF_BANK:(half + 1) * HALF_BANK].rearrange(
                                   "p (w1 c21 c0 r) -> p c0 c21 w1 r", w1=2, c21=4, c0=2))
            live["du_sb", h] = du_sb

        def flip_du(h, b):
            flipped = bank(b)
            for half in range(2):
                for c0 in range(2):
                    nc.tensor.transpose(
                        flipped[:].rearrange("p (jw c0 half jh) -> p c0 half jw jh", jw=16, c0=2, half=2)[:, c0, half],
                        live["du_sb", h][:, half, c0 * P:(c0 + 1) * P], perm_du[:])
            live["du_flipped", h] = flipped

        def swap_du(h):
            du_rows = work.tile([P, 512], F32, name="du_rows", bufs=2, align_bytes=64)
            nc.vector.transpose(out=du_rows[:], in_=live["du_flipped", h][:])
            live["du_rows", h] = du_rows

        def spread_du(h, k, engines):
            spread = work.tile([P, 2, 512], F32, name="spread", bufs=5)
            values = live["du_rows", h][:].rearrange("p (pair k e) -> p k pair e", k=4, e=2)[:, k]
            rows = len(engines)
            for row in range(rows):
                times(engines[row], spread[:, row, :].rearrange("p (pair e b) -> p pair e b", e=2, b=4),
                      values.unsqueeze(3).to_broadcast([P, 64, 2, 4]), MEAN_16)
            written = spread[:].rearrange("p r w -> p (r w)")[:, 0:rows * 512]
            nc.sync.dma_start(out=out_0_rows[4 * h + k].rearrange("p (n w) -> p n w", w=rows * 512),
                              in_=written.unsqueeze(1).to_broadcast([P, 4 // rows, rows * 512]))

        def pool_x(c):
            if c % 2 == 0:
                live["pooled", c // 2] = bank(FIRST_POOL_BANK + c // 2)
            rows_held = 2 if c >= FIRST_PAIRED else 1
            matrix = pool_pairs if c >= FIRST_PAIRED else pool_rows
            sums = live["pooled", c // 2][:].rearrange("p (c kh q j v r) -> p c q v kh j r",
                                                       c=2, kh=8, j=rows_held, v=2, r=4)
            for q in range(4 // rows_held):
                for v in range(2):
                    for n in range(2 * rows_held):
                        row, b0 = divmod(n, 2)
                        at = row * 512 + v * 256
                        nc.tensor.matmul(sums[:, c % 2, q, v], lhsT=x_sb[c][:, q, at + b0:at + 256:2],
                                         rhs=matrix[:].rearrange("p (kh j r) -> p kh j r", j=rows_held, r=4),
                                         start=(n == 0), stop=(n == 2 * rows_held - 1))

        pair_sums = keep.tile([P, 2048], F32, name="pair_sums", align_bytes=64)
        u_bf = keep.tile([P, 1024], BF16, name="u_bf")

        def swap_pooled(n):
            nc.vector.transpose(out=pair_sums[:, n * 512:(n + 1) * 512], in_=live["pooled", n][:])

        def add_pooled():
            pairs = pair_sums[:].rearrange("p (c h k z w0 e b) -> p z w0 b c h k e",
                                           c=CHANNELS, h=2, k=4, z=4, w0=2, e=2)
            result = u_bf[:].rearrange("p (z h c w0 k e) -> p z w0 c h k e", z=4, h=2, c=CHANNELS, w0=2, k=4)
            for z in range(4):
                for w0 in range(2):
                    nc.vector.tensor_tensor(out=result[:, z, w0], in0=pairs[:, z, w0, 0], in1=pairs[:, z, w0, 1],
                                            op=ALU.add)

        def flip_and_weave_u(b):
            flipped = bank(b)
            for z in range(4):
                nc.tensor.transpose(flipped[:, z * P:(z + 1) * P], u_bf[:].bitcast(F32)[:, z * P:(z + 1) * P], perm_u[:])
            woven = keep.tile([P, 1024], BF16, name="woven_u", align_bytes=64)
            nc.scalar.copy(out=woven[:].bitcast(F32).rearrange("p (j z) -> p j z", z=4),
                           in_=flipped[:].rearrange("p (z j) -> p j z", z=4))
            live["woven_u"] = woven

        def quantize_u():
            real = slice(HALF_BANK, 2 * HALF_BANK)
            nc.vector.quantize_mx(out=u_codes[:, real].bitcast(E4M3X4), scales=u_scales[:, real],
                                  in_=live["woven_u"][:])

        def flip_dz(g, pair, b):
            flipped = bank(b)
            words = dz[g][:].rearrange("p t w1 h n -> p (t w1 h n)").bitcast(F32)
            for n in range(4):
                at = (4 * pair + n) * P
                nc.tensor.transpose(flipped[:, n * P:(n + 1) * P], words[:, at:at + P], ident[:])
            live["dz_flipped", g, pair] = flipped

        def weave_dz_n(g, pair, engine):
            if pair == 0:
                live["woven_n", g] = work.tile([P, 2048], BF16, name="woven_n", bufs=4, align_bytes=64)
            words = live["woven_n", g][:].bitcast(F32)[:, pair * 512:(pair + 1) * 512]
            copy(engine, words.rearrange("p (t l w1) -> p t l w1", t=2, w1=2),
                 live["dz_flipped", g, pair][:].rearrange("p (t w1 l) -> p t l w1", t=2, w1=2))

        def quantize_dz_n(g):
            codes = work.tile([P, 512], U32, name="dz_n_codes", bufs=5, align_bytes=64)
            scales = work.tile([P, 512], U8, name="dz_n_scales", bufs=5, align_bytes=64)
            nc.vector.quantize_mx(out=codes[:].bitcast(E5M2X4), scales=scales[:], in_=live["woven_n", g][:])
            live["dz_n", g] = (codes, scales)

        def multiply_n(g, pair, b):
            codes, scales = live["dz_n", g]
            sums = bank(b)
            for half in range(2):
                ls = slice((2 * pair + half) * P, (2 * pair + half + 1) * P)
                window = slice((1 - half) * HALF_BANK, (3 - half) * HALF_BANK)
                nc.tensor.matmul_mx(out=sums[:], lhsT=codes[:, ls].bitcast(E5M2X4), lhsT_scale=scales[:, ls],
                                    rhs=u_codes[:, window].bitcast(E4M3X4), rhs_scale=u_scales[:, window],
                                    start=(half == 0), stop=(half == 1))
            live["da", g, pair] = sums

        def copy_da(g, pair, engine):
            if pair == 0:
                live["da_sb", g] = work.tile([P, 1024], F32, name="da_sb", tag="x_then_da", bufs=CHANNELS)
            copy(engine, live["da_sb", g][:, pair * 512:(pair + 1) * 512], live["da", g, pair][:])
            if pair == 1:
                nc.sync.dma_start(out=out_1_rows[g], in_=live["da_sb", g][:])

        one_row, two_rows, two_rows_shared = ("scalar",), ("scalar", "scalar"), ("scalar", "vector")

        for t in range(4):
            sort_grad(0, 0, t)
            flip_grad(0, 0, t, FIRST_POOL_BANK + t)
            divide(0, 0, t, "vector")
        weave_att(0, 0)
        weave_dz(0, 0, 0, "vector")

        pool_steps = (2, 4, 5, 6)
        for step in range(8):
            s, i = divmod(step, 4)
            following = ((0, 1), (1, 0))[s]
            sort_grad(*following, i)
            if step < 7:
                weave_att(*divmod(step + 1, 4))
            flip_grad(*following, i, 1 + step % 3)
            if step > 0:
                multiply_l(0, *divmod(step - 1, 4))
            if step in pool_steps:
                pool_x(pool_steps.index(step))
            if i < 3:
                weave_dz(0, s, i + 1, "vector")
            quantize_dz_l(0, s, i)
            quantize_att(s, i)
            divide(*following, i, "vector")
            if i == 3:
                weave_dz(*following, 0, "vector")
        multiply_l(0, 1, 3)

        sort_grad(1, 1, 0)
        sort_grad(1, 1, 1)
        copy_du(0)
        sort_grad(1, 1, 2)
        sort_grad(1, 1, 3)
        flip_grad(1, 1, 0, 3)
        flip_grad(1, 1, 1, 7)
        flip_du(0, 0)
        flip_grad(1, 1, 2, 2)
        pool_x(4)
        weave_dz(1, 0, 1, "vector")
        quantize_dz_l(1, 0, 0)
        swap_du(0)
        divide(1, 1, 0, "vector")
        flip_grad(1, 1, 3, 3)

        for i in range(1, 4):
            spread_du(0, i - 1, one_row)
            multiply_l(1, 0, i - 1)
            if i == 2:
                pool_x(5)
            if i < 3:
                weave_dz(1, 0, i + 1, "vector")
                divide(1, 1, i, "scalar")
            else:
                divide(1, 1, 3, "vector")
            quantize_dz_l(1, 0, i)
        multiply_l(1, 0, 3)

        flip_dz(0, 0, 0)
        flip_dz(0, 1, 2)
        weave_dz(1, 1, 0, "vector")
        weave_dz(1, 1, 3, "scalar")
        spread_du(0, 3, one_row)
        weave_dz_n(0, 0, "scalar")
        weave_dz_n(0, 1, "scalar")
        for i in range(4):
            if i < 2:
                weave_dz(1, 1, i + 1, "vector")
            quantize_dz_l(1, 1, i)
            multiply_l(1, 1, i)

        copy_du(1)
        pool_x(6)
        for n in range(3):
            swap_pooled(n)
        quantize_dz_n(0)
        flip_du(1, 0)
        pool_x(7)
        flip_dz(2, 0, 3)
        flip_dz(2, 1, 2)
        swap_du(1)
        spread_du(1, 0, two_rows_shared)
        swap_pooled(3)
        weave_dz_n(2, 0, "scalar")
        weave_dz_n(2, 1, "scalar")
        flip_dz(4, 0, 3)
        flip_dz(4, 1, 1)
        spread_du(1, 1, two_rows)
        add_pooled()
        flip_dz(6, 0, 4)
        flip_dz(6, 1, 5)
        flip_and_weave_u(6)
        quantize_dz_n(2)
        weave_dz_n(4, 0, "vector")
        quantize_u()
        weave_dz_n(4, 1, "scalar")
        spread_du(1, 2, two_rows_shared)
        weave_dz_n(6, 0, "vector")
        weave_dz_n(6, 1, "scalar")
        quantize_dz_n(4)

        order = (0, 2, 4, 6, 1, 3, 5, 7)
        for n, g in enumerate(order):
            multiply_n(g, 0, 2 * (n % 2))
            multiply_n(g, 1, 2 * (n % 2) + 1)
            if n + 4 < PASSES:
                flip_dz(order[n + 4], 0, 4 + (2 * n + 3) % 4)
                flip_dz(order[n + 4], 1, 4 + (2 * n) % 4)
            if n == 0:
                spread_du(1, 3, two_rows_shared)
            if n + 3 < PASSES:
                quantize_dz_n(order[n + 3])
            copy_da(g, 0, "scalar")
            copy_da(g, 1, "vector")
            if n + 4 < PASSES:
                weave_dz_n(order[n + 4], 0, "scalar")
                weave_dz_n(order[n + 4], 1, "vector" if n % 2 == 0 else "scalar")
